import numpy as np
import ml_dtypes


def mxq(x, axis, fmt="e4m3"):
    dtype, down = {"e4m3": (ml_dtypes.float8_e4m3fn, 7), "e5m2": (ml_dtypes.float8_e5m2, 14)}[fmt]
    v = np.moveaxis(np.asarray(x, np.float32).astype(ml_dtypes.bfloat16).astype(np.float64), axis, -1)
    blocks = v.reshape(v.shape[:-1] + (-1, 32))
    amax = np.abs(blocks).max(-1, keepdims=True)
    byte = np.maximum(np.where(amax > 0, np.frexp(amax)[1] - 1 + 127, 0) - down, 1)
    scale = np.exp2(byte - 127.0)
    codes = (blocks / scale).astype(np.float32).astype(dtype).astype(np.float64)
    return np.moveaxis((codes * scale).reshape(v.shape), -1, axis)


WIDE = False


def mx_kscale(k):
    if not WIDE:
        return np.ones(k)
    levels = np.array([10, -10, 5, -5, 0])
    a = np.random.permutation(np.resize(levels, k // 512 * 4)).reshape(k // 512, 4)
    idx = np.arange(k)
    return np.exp2(a[idx // 512, idx % 128 // 32])


BF16 = ml_dtypes.bfloat16


def bf(x):
    return np.asarray(x, np.float32).astype(BF16)


def f64(x):
    return np.asarray(x).astype(np.float64)


E2M1 = np.array([0.0, 0.5, 1.0, 1.5, 2.0, 3.0, 4.0, 6.0, -0.0, -0.5, -1.0, -1.5, -2.0, -3.0, -4.0, -6.0])


def pack_weight(w, fmt):
    k, n = w.shape
    w = f64(bf(w)).reshape(k // 32, 32, n)
    amax = np.abs(w).max(1)
    if fmt == "e4m3":
        byte = np.frexp(amax)[1] - 1 + 127 - 7
    else:
        mant, ex = np.frexp(amax / 6.0)
        byte = np.where(mant > 0.5, ex, ex - 1) + 127
    byte = np.clip(np.where(amax > 0, byte, 1), 1, 254)
    scaled = (w * np.exp2(127.0 - byte)[:, None, :]).reshape(k, n).astype(np.float32)
    by_word = np.ascontiguousarray(scaled.reshape(k // 512, 128, 4, n).transpose(0, 1, 3, 2))
    if fmt == "e4m3":
        words = by_word.astype(ml_dtypes.float8_e4m3fn).view(np.uint8)
    else:
        c = by_word.astype(ml_dtypes.float4_e2m1fn).view(np.uint8) & 0xF
        words = c[..., 0::2] | (c[..., 1::2] << 4)
    return np.ascontiguousarray(words), np.ascontiguousarray(byte.astype(np.uint8).reshape(k // 512, 16, n))


def unpack_weight(words, scales, fmt):
    g, p, n, _ = words.shape
    if fmt == "e4m3":
        vals = np.ascontiguousarray(words).view(ml_dtypes.float8_e4m3fn).astype(np.float64)
    else:
        nib = np.empty((g, p, n, 4), np.uint8)
        nib[..., 0::2] = words & 0xF
        nib[..., 1::2] = words >> 4
        vals = E2M1[nib]
    vals = vals * np.repeat(np.exp2(scales.astype(np.float64) - 127.0), 8, axis=1)[..., None]
    return vals.transpose(0, 1, 3, 2).reshape(g * 512, n)


B, E, D = 256, 2048, 2048


def setup_inputs():
    s = mx_kscale(E)
    ws = 1.0 / np.sqrt(E)
    inputs = {
        "x": bf(np.random.standard_normal((B, E)) * s),
        "state_A": bf(np.random.uniform(0.0, 1.0, (B, D))),
        "state_B": bf(0.5 + np.random.uniform(0.0, 1.0, (B, D))),
        "state_p": bf(np.random.standard_normal((B, D))),
        "state_x": bf(np.random.standard_normal((B, E)) * s),
        "time_decay": bf(0.5 * np.random.standard_normal(D)),
        "time_first": bf(np.log(0.3) + 0.3 * np.random.standard_normal(D)),
        "time_mix_k": bf(np.random.uniform(0.0, 1.0, (1, E))),
        "time_mix_v": bf(np.random.uniform(0.0, 1.0, (1, E))),
    }
    w_key = np.random.standard_normal((D, E)) * ws / s[None, :]
    w_value = np.random.standard_normal((D, E)) * ws / s[None, :]
    inputs["W_key_words"], inputs["W_key_scales"] = pack_weight(np.ascontiguousarray(w_key.T), "e4m3")
    inputs["W_value_words"], inputs["W_value_scales"] = pack_weight(np.ascontiguousarray(w_value.T), "e4m3")
    return inputs


def reference(x, state_A, state_B, state_p, state_x, time_decay, time_first, time_mix_k, time_mix_v, W_key_words, W_key_scales, W_value_words, W_value_scales):
    x, state_x = f64(x), f64(state_x)
    state_A, state_B, state_p = f64(state_A), f64(state_B), f64(state_p)
    mk, mv = f64(time_mix_k), f64(time_mix_v)
    xk = x * mk + state_x * (1.0 - mk)
    xv = x * mv + state_x * (1.0 - mv)
    k = mxq(xk, 1, "e4m3") @ unpack_weight(W_key_words, W_key_scales, "e4m3")
    v = mxq(xv, 1, "e4m3") @ unpack_weight(W_value_words, W_value_scales, "e4m3")
    ww = f64(time_first) + k
    p = np.maximum(state_p, ww)
    e1 = np.exp(state_p - p)
    e2 = np.exp(ww - p)
    a = e1 * state_A + e2 * v
    b = e1 * state_B + e2
    td = -np.exp(f64(time_decay))
    ww = state_p + td
    p = np.maximum(ww, k)
    e1 = np.exp(ww - p)
    e2 = np.exp(k - p)
    new_A = e1 * state_A + e2 * v
    new_B = e1 * state_B + e2
    return (a, b, new_A, new_B, p)

@@ -1,0 +1,240 @@
+import concourse.mybir as mybir
+from concourse.masks import make_identity
+
+F32 = mybir.dt.float32
+BF16 = mybir.dt.bfloat16
+I32 = mybir.dt.int32
+U32 = mybir.dt.uint32
+U8 = mybir.dt.uint8
+FP8X4 = mybir.dt.float8_e4m3fn_x4
+ALU = mybir.AluOpType
+ACT = mybir.ActivationFunctionType
+
+P = 128
+B = 256
+E = 2048
+D = 2048
+PACK = 4
+K_PASS = P * PACK
+PASSES = E // K_PASS
+ROW_TILES = B // P
+N_BLOCK = 512
+N_BLOCKS = D // N_BLOCK
+QUADRANTS = 4
+
+FLOPS = 2 * 2 * B * E * D
+
+
+def tile_rwkv_timemix_for_quant_pa_kernel(
+    tc,
+    x,
+    state_A,
+    state_B,
+    state_p,
+    state_x,
+    time_decay,
+    time_first,
+    time_mix_k,
+    time_mix_v,
+    W_key_words,
+    W_key_scales,
+    W_value_words,
+    W_value_scales,
+    out_0,
+    out_1,
+    out_2,
+    out_3,
+    out_4,
+):
+    nc = tc.nc
+    weights = ((W_key_words, W_key_scales), (W_value_words, W_value_scales))
+
+    with tc.tile_pool(name="keep", bufs=1) as keep, tc.psum_pool(name="sums", bufs=2) as sums:
+        ident = keep.tile([P, P], BF16)
+        make_identity(nc, ident[:])
+
+        w_words = keep.tile([P, 2, PASSES, D], U32, align_bytes=64)
+        w_scales = keep.tile([P, 2, D], U8, align_bytes=64)
+        nc.vector.memset(w_scales[:].bitcast(I32), 0)
+        x_codes = keep.tile([P, PASSES, 2, B], U32, align_bytes=64)
+        x_scales = keep.tile([P, PASSES, 2, B], U8, align_bytes=64)
+        ab_sb = keep.tile([P, 2, ROW_TILES, D], BF16)
+        sp_sb = keep.tile([P, ROW_TILES, D], BF16)
+        shift = keep.tile([P, 2, D], F32)
+        uw = keep.tile([P, ROW_TILES, 2, D], F32)
+        mix_bf = keep.tile([P, 2, PASSES, PACK], BF16)
+        mix = keep.tile([P, 2, PASSES * PACK], F32)
+        rest = keep.tile([P, 2, PASSES * PACK], F32)
+
+        with tc.tile_pool(name="inputs", bufs=1) as inputs, tc.tile_pool(
+            name="mixing", bufs=2
+        ) as mixing, tc.psum_pool(name="turned", bufs=2) as turned:
+            x_sb = inputs.tile([P, ROW_TILES, E], BF16)
+            sx_sb = inputs.tile([P, ROW_TILES, E], BF16)
+            tf_all = inputs.tile([P, D], BF16)
+            td_all = inputs.tile([P, D], BF16)
+
+            x_rows = x.rearrange("(m p) e -> p m e", p=P)
+            sx_rows = state_x.rearrange("(m p) e -> p m e", p=P)
+
+            def load_x(g):
+                k_cols = slice(K_PASS * g, K_PASS * (g + 1))
+                nc.sync.dma_start(out=x_sb[:, :, k_cols], in_=x_rows[:, :, k_cols])
+                nc.sync.dma_start(out=sx_sb[:, :, k_cols], in_=sx_rows[:, :, k_cols])
+
+            for s, time_mix in enumerate((time_mix_k, time_mix_v)):
+                nc.sync.dma_start(
+                    out=mix_bf[:, s], in_=time_mix[0].rearrange("(g p t) -> p g t", g=PASSES, p=P)
+                )
+            load_x(0)
+            nc.sync.dma_start(out=tf_all[:], in_=time_first.partition_broadcast(P))
+            nc.sync.dma_start(out=sp_sb[:, 0, :], in_=state_p[0:P, :])
+            nc.sync.dma_start(out=td_all[:], in_=time_decay.partition_broadcast(P))
+            load_x(1)
+            nc.sync.dma_start(out=sp_sb[:, 1, :], in_=state_p[P : 2 * P, :])
+            load_x(2)
+            load_x(3)
+            for s in range(2):
+                for quad in range(QUADRANTS):
+                    nc.sync.dma_start(
+                        out=w_scales[32 * quad : 32 * quad + 16, s, :].bitcast(I32),
+                        in_=weights[s][1][:, 4 * quad : 4 * quad + 4, :].bitcast(I32),
+                    )
+            for j in range(N_BLOCKS):
+                n_cols = slice(N_BLOCK * j, N_BLOCK * (j + 1))
+                for s in range(2):
+                    words = weights[s][0].rearrange("g p n t -> p g (n t)")
+                    nc.sync.dma_start(
+                        out=w_words[:, s, :, n_cols].bitcast(I32),
+                        in_=words[:, :, PACK * N_BLOCK * j : PACK * N_BLOCK * (j + 1)].bitcast(I32),
+                    )
+                for s, state in enumerate((state_A, state_B)):
+                    nc.sync.dma_start(
+                        out=ab_sb[:, s, :, n_cols],
+                        in_=state.rearrange("(m p) n -> p m n", p=P)[:, :, n_cols],
+                    )
+
+            nc.vector.tensor_copy(out=mix[:], in_=mix_bf[:].rearrange("p s g t -> p s (g t)"))
+            nc.vector.tensor_scalar(
+                out=rest[:],
+                in0=mix_bf[:].rearrange("p s g t -> p s (g t)"),
+                scalar1=-1.0,
+                scalar2=1.0,
+                op0=ALU.mult,
+                op1=ALU.add,
+            )
+            for g in range(PASSES):
+                x_turned = turned.tile([P, PACK, B], BF16)
+                sx_turned = turned.tile([P, PACK, B], BF16)
+                for t in range(PACK):
+                    k_cols = slice(K_PASS * g + t, K_PASS * (g + 1), PACK)
+                    for m in range(ROW_TILES):
+                        rows = slice(P * m, P * (m + 1))
+                        nc.tensor.transpose(x_turned[:, t, rows], x_sb[:, m, k_cols], ident[:])
+                        nc.tensor.transpose(sx_turned[:, t, rows], sx_sb[:, m, k_cols], ident[:])
+                sx_share = mixing.tile([P, 2, PACK, B], F32)
+                planes = mixing.tile([P, 2, PACK, B], BF16)
+                for s in range(2):
+                    for t in range(PACK):
+                        col = PACK * g + t
+                        nc.scalar.activation(
+                            out=sx_share[:, s, t, :],
+                            in_=sx_turned[:, t, :],
+                            func=ACT.Copy,
+                            scale=rest[:, s, col : col + 1],
+                        )
+                        nc.vector.scalar_tensor_tensor(
+                            out=planes[:, s, t, :],
+                            in0=x_turned[:, t, :],
+                            scalar=mix[:, s, col : col + 1],
+                            in1=sx_share[:, s, t, :],
+                            op0=ALU.mult,
+                            op1=ALU.add,
+                        )
+                grouped = mixing.tile([P, 2, B, PACK], BF16, align_bytes=64)
+                for s in range(2):
+                    nc.vector.tensor_copy(
+                        out=grouped[:, s].rearrange("p (c i) t -> p c t i", i=4),
+                        in_=planes[:, s].rearrange("p t (c i) -> p c t i", i=4),
+                    )
+                nc.vector.quantize_mx(
+                    out=x_codes[:, g].rearrange("p s b -> p (s b)").bitcast(FP8X4),
+                    scales=x_scales[:, g].rearrange("p s b -> p (s b)"),
+                    in_=grouped[:].rearrange("p s b t -> p (s b t)"),
+                )
+
+            for j in range(N_BLOCKS):
+                n_cols = slice(N_BLOCK * j, N_BLOCK * (j + 1))
+                nc.scalar.activation(out=shift[:, 0, n_cols], in_=tf_all[:, n_cols], func=ACT.Copy)
+                nc.scalar.activation(out=shift[:, 1, n_cols], in_=td_all[:, n_cols], func=ACT.Exp)
+
+        for j in range(N_BLOCKS):
+            n_cols = slice(N_BLOCK * j, N_BLOCK * (j + 1))
+            for m in range(ROW_TILES):
+                nc.gpsimd.tensor_tensor(
+                    out=uw[:, m, :, n_cols],
+                    in0=sp_sb[:, m, n_cols].unsqueeze(1).to_broadcast([P, 2, N_BLOCK]),
+                    in1=shift[:, :, n_cols],
+                    op=ALU.subtract,
+                )
+
+        with tc.tile_pool(name="work", bufs=3, reuse_waits="tile") as work, tc.psum_pool(
+            name="staged", bufs=3, reuse_waits="tile"
+        ) as staged:
+            for j in range(N_BLOCKS):
+                n_cols = slice(N_BLOCK * j, N_BLOCK * (j + 1))
+                for m in range(ROW_TILES):
+                    rows = slice(P * m, P * (m + 1))
+                    k_ps = sums.tile([P, N_BLOCK], F32)
+                    v_ps = sums.tile([P, N_BLOCK], F32)
+                    for s, product in enumerate((k_ps, v_ps)):
+                        for g in range(PASSES):
+                            nc.tensor.matmul_mx(
+                                out=product[:],
+                                lhsT=x_codes[:, g, s, rows].bitcast(FP8X4),
+                                lhsT_scale=x_scales[:, g, s, rows],
+                                rhs=w_words[:, s, g, n_cols].bitcast(FP8X4),
+                                rhs_scale=w_scales[4 * g : P, s, n_cols],
+                                start=(g == 0),
+                                stop=(g == PASSES - 1),
+                            )
+                    ab_ps = staged.tile([P, 2, N_BLOCK], BF16)
+                    for s in range(2):
+                        nc.tensor.matmul(
+                            out=ab_ps[:, s, :], lhsT=ident[:], rhs=ab_sb[:, s, m, n_cols], start=True, stop=True
+                        )
+
+                    first = work.tile([P, 2, N_BLOCK], F32)
+                    nc.vector.tensor_tensor(
+                        out=first[:],
+                        in0=uw[:, m, :, n_cols],
+                        in1=k_ps[:].unsqueeze(1).to_broadcast([P, 2, N_BLOCK]),
+                        op=ALU.subtract,
+                    )
+                    new_p = work.tile([P, N_BLOCK], F32)
+                    nc.vector.tensor_tensor(out=new_p[:], in0=uw[:, m, 1, n_cols], in1=k_ps[:], op=ALU.max)
+                    nc.sync.dma_start(out=out_4[rows, n_cols], in_=new_p[:])
+
+                    second = work.tile([P, 2, 2, N_BLOCK], F32)
+                    nc.scalar.activation(out=second[:, :, 1, :], in_=first[:], func=ACT.Relu)
+                    nc.scalar.activation(out=first[:], in_=first[:], func=ACT.Exp)
+                    nc.scalar.activation(out=second[:, :, 1, :], in_=second[:, :, 1, :], func=ACT.Exp, scale=-1.0)
+                    nc.vector.tensor_tensor(
+                        out=second[:, :, 0, :],
+                        in0=second[:, :, 1, :],
+                        in1=v_ps[:].unsqueeze(1).to_broadcast([P, 2, N_BLOCK]),
+                        op=ALU.mult,
+                    )
+                    result = work.tile([P, 2, 2, N_BLOCK], F32)
+                    for h, (out_a, out_b) in enumerate(((out_0, out_1), (out_2, out_3))):
+                        nc.vector.scalar_tensor_tensor(
+                            out=result[:, h],
+                            in0=first[:, h, :].unsqueeze(1).to_broadcast([P, 2, N_BLOCK]),
+                            scalar=1.0,
+                            in1=ab_ps[:],
+                            op0=ALU.min,
+                            op1=ALU.mult,
+                        )
+                        nc.gpsimd.tensor_tensor(out=result[:, h], in0=result[:, h], in1=second[:, h], op=ALU.add)
+                        nc.sync.dma_start(out=out_a[rows, n_cols], in_=result[:, h, 0, :])
+                        nc.sync.dma_start(out=out_b[rows, n_cols], in_=result[:, h, 1, :])

@@ -20,6 +20,7 @@ PASSES = E // K_PASS
 ROW_TILES = B // P
 N_BLOCK = 512
 N_BLOCKS = D // N_BLOCK
+UNITS = N_BLOCKS * ROW_TILES
 QUADRANTS = 4
 
 FLOPS = 2 * 2 * B * E * D
@@ -48,20 +49,24 @@ def tile_rwkv_timemix_for_quant_pa_kernel(
 ):
     nc = tc.nc
     weights = ((W_key_words, W_key_scales), (W_value_words, W_value_scales))
+    assert N_BLOCKS == PASSES
 
-    with tc.tile_pool(name="keep", bufs=1) as keep, tc.psum_pool(name="sums", bufs=2) as sums:
+    def n_cols(j):
+        return slice(N_BLOCK * j, N_BLOCK * (j + 1))
+
+    with tc.manual_schedule(), tc.tile_pool(name="keep", bufs=1) as keep, tc.psum_pool(name="sums", bufs=2) as sums:
         ident = keep.tile([P, P], BF16)
         make_identity(nc, ident[:])
 
-        w_words = keep.tile([P, 2, PASSES, D], U32, align_bytes=64)
+        w_words = keep.tile([P, N_BLOCKS, 2, PASSES, N_BLOCK], U32, align_bytes=64)
         w_scales = keep.tile([P, 2, D], U8, align_bytes=64)
         nc.vector.memset(w_scales[:].bitcast(I32), 0)
         x_codes = keep.tile([P, PASSES, 2, B], U32, align_bytes=64)
         x_scales = keep.tile([P, PASSES, 2, B], U8, align_bytes=64)
-        ab_sb = keep.tile([P, 2, ROW_TILES, D], BF16)
-        sp_sb = keep.tile([P, ROW_TILES, D], BF16)
-        shift = keep.tile([P, 2, D], F32)
-        uw = keep.tile([P, ROW_TILES, 2, D], F32)
+        ab_sb = keep.tile([P, N_BLOCKS, 2, ROW_TILES, N_BLOCK], BF16)
+        sp_sb = keep.tile([P, N_BLOCKS, ROW_TILES, N_BLOCK], BF16)
+        shift = keep.tile([P, N_BLOCKS, 2, N_BLOCK], F32)
+        uw = keep.tile([P, N_BLOCKS, ROW_TILES, 2, N_BLOCK], F32)
         mix_bf = keep.tile([P, 2, PASSES, PACK], BF16)
         mix = keep.tile([P, 2, PASSES * PACK], F32)
         rest = keep.tile([P, 2, PASSES * PACK], F32)
@@ -69,31 +74,26 @@ def tile_rwkv_timemix_for_quant_pa_kernel(
         with tc.tile_pool(name="inputs", bufs=1) as inputs, tc.tile_pool(
             name="mixing", bufs=2
         ) as mixing, tc.psum_pool(name="turned", bufs=2) as turned:
-            x_sb = inputs.tile([P, ROW_TILES, E], BF16)
-            sx_sb = inputs.tile([P, ROW_TILES, E], BF16)
-            tf_all = inputs.tile([P, D], BF16)
-            td_all = inputs.tile([P, D], BF16)
+            x_sb = inputs.tile([P, PASSES, ROW_TILES, K_PASS], BF16)
+            sx_sb = inputs.tile([P, PASSES, ROW_TILES, K_PASS], BF16)
+            lone_rows = inputs.tile([P, 2, D], BF16)
+            nc.vector.memset(lone_rows[:].bitcast(I32), 0)
+            ones = inputs.tile([P, P], BF16)
+            nc.vector.memset(ones[:], 1.0)
 
-            x_rows = x.rearrange("(m p) e -> p m e", p=P)
-            sx_rows = state_x.rearrange("(m p) e -> p m e", p=P)
-
-            def load_x(g):
+            by_row_tile = "(m p) c -> p m c"
+            for g in range(PASSES):
                 k_cols = slice(K_PASS * g, K_PASS * (g + 1))
-                nc.sync.dma_start(out=x_sb[:, :, k_cols], in_=x_rows[:, :, k_cols])
-                nc.sync.dma_start(out=sx_sb[:, :, k_cols], in_=sx_rows[:, :, k_cols])
-
-            for s, time_mix in enumerate((time_mix_k, time_mix_v)):
-                nc.sync.dma_start(
-                    out=mix_bf[:, s], in_=time_mix[0].rearrange("(g p t) -> p g t", g=PASSES, p=P)
-                )
-            load_x(0)
-            nc.sync.dma_start(out=tf_all[:], in_=time_first.partition_broadcast(P))
-            nc.sync.dma_start(out=sp_sb[:, 0, :], in_=state_p[0:P, :])
-            nc.sync.dma_start(out=td_all[:], in_=time_decay.partition_broadcast(P))
-            load_x(1)
-            nc.sync.dma_start(out=sp_sb[:, 1, :], in_=state_p[P : 2 * P, :])
-            load_x(2)
-            load_x(3)
+                nc.sync.dma_start(out=x_sb[:, g], in_=x.rearrange(by_row_tile, p=P)[:, :, k_cols])
+                nc.sync.dma_start(out=sx_sb[:, g], in_=state_x.rearrange(by_row_tile, p=P)[:, :, k_cols])
+                if g == 0:
+                    for s, time_mix in enumerate((time_mix_k, time_mix_v)):
+                        nc.sync.dma_start(
+                            out=mix_bf[:, s], in_=time_mix[0].rearrange("(g p t) -> p g t", g=PASSES, p=P)
+                        )
+                    for s, vector in enumerate((time_first, time_decay)):
+                        nc.sync.dma_start(out=lone_rows[0:1, s, :], in_=vector.unsqueeze(0))
+                nc.sync.dma_start(out=sp_sb[:, g], in_=state_p.rearrange(by_row_tile, p=P)[:, :, n_cols(g)])
             for s in range(2):
                 for quad in range(QUADRANTS):
                     nc.sync.dma_start(
@@ -101,18 +101,14 @@ def tile_rwkv_timemix_for_quant_pa_kernel(
                         in_=weights[s][1][:, 4 * quad : 4 * quad + 4, :].bitcast(I32),
                     )
             for j in range(N_BLOCKS):
-                n_cols = slice(N_BLOCK * j, N_BLOCK * (j + 1))
                 for s in range(2):
                     words = weights[s][0].rearrange("g p n t -> p g (n t)")
                     nc.sync.dma_start(
-                        out=w_words[:, s, :, n_cols].bitcast(I32),
+                        out=w_words[:, j, s].bitcast(I32),
                         in_=words[:, :, PACK * N_BLOCK * j : PACK * N_BLOCK * (j + 1)].bitcast(I32),
                     )
                 for s, state in enumerate((state_A, state_B)):
-                    nc.sync.dma_start(
-                        out=ab_sb[:, s, :, n_cols],
-                        in_=state.rearrange("(m p) n -> p m n", p=P)[:, :, n_cols],
-                    )
+                    nc.sync.dma_start(out=ab_sb[:, j, s], in_=state.rearrange(by_row_tile, p=P)[:, :, n_cols(j)])
 
             nc.vector.tensor_copy(out=mix[:], in_=mix_bf[:].rearrange("p s g t -> p s (g t)"))
             nc.vector.tensor_scalar(
@@ -123,15 +119,18 @@ def tile_rwkv_timemix_for_quant_pa_kernel(
                 op0=ALU.mult,
                 op1=ALU.add,
             )
-            for g in range(PASSES):
+
+            def turn(g):
                 x_turned = turned.tile([P, PACK, B], BF16)
                 sx_turned = turned.tile([P, PACK, B], BF16)
                 for t in range(PACK):
-                    k_cols = slice(K_PASS * g + t, K_PASS * (g + 1), PACK)
                     for m in range(ROW_TILES):
                         rows = slice(P * m, P * (m + 1))
-                        nc.tensor.transpose(x_turned[:, t, rows], x_sb[:, m, k_cols], ident[:])
-                        nc.tensor.transpose(sx_turned[:, t, rows], sx_sb[:, m, k_cols], ident[:])
+                        nc.tensor.transpose(x_turned[:, t, rows], x_sb[:, g, m, t:K_PASS:PACK], ident[:])
+                        nc.tensor.transpose(sx_turned[:, t, rows], sx_sb[:, g, m, t:K_PASS:PACK], ident[:])
+                return x_turned, sx_turned
+
+            def mix_pass(g, x_turned, sx_turned):
                 sx_share = mixing.tile([P, 2, PACK, B], F32)
                 planes = mixing.tile([P, 2, PACK, B], BF16)
                 for s in range(2):
@@ -151,90 +150,132 @@ def tile_rwkv_timemix_for_quant_pa_kernel(
                             op0=ALU.mult,
                             op1=ALU.add,
                         )
+                return planes
+
+            def regroup(planes):
                 grouped = mixing.tile([P, 2, B, PACK], BF16, align_bytes=64)
                 for s in range(2):
                     nc.vector.tensor_copy(
                         out=grouped[:, s].rearrange("p (c i) t -> p c t i", i=4),
                         in_=planes[:, s].rearrange("p t (c i) -> p c t i", i=4),
                     )
+                return grouped
+
+            def quantise(g, grouped):
                 nc.vector.quantize_mx(
                     out=x_codes[:, g].rearrange("p s b -> p (s b)").bitcast(FP8X4),
                     scales=x_scales[:, g].rearrange("p s b -> p (s b)"),
                     in_=grouped[:].rearrange("p s b t -> p (s b t)"),
                 )
 
-            for j in range(N_BLOCKS):
-                n_cols = slice(N_BLOCK * j, N_BLOCK * (j + 1))
-                nc.scalar.activation(out=shift[:, 0, n_cols], in_=tf_all[:, n_cols], func=ACT.Copy)
-                nc.scalar.activation(out=shift[:, 1, n_cols], in_=td_all[:, n_cols], func=ACT.Exp)
+            def spread(j):
+                banks = []
+                for s in range(2):
+                    spread_ps = sums.tile([P, N_BLOCK], F32, tag=("k_ps", "v_ps")[s])
+                    nc.tensor.matmul(
+                        out=spread_ps[:], lhsT=ones[:], rhs=lone_rows[:, s, n_cols(j)], start=True, stop=True
+                    )
+                    banks.append(spread_ps)
+                return banks
 
-        for j in range(N_BLOCKS):
-            n_cols = slice(N_BLOCK * j, N_BLOCK * (j + 1))
-            for m in range(ROW_TILES):
-                nc.gpsimd.tensor_tensor(
-                    out=uw[:, m, :, n_cols],
-                    in0=sp_sb[:, m, n_cols].unsqueeze(1).to_broadcast([P, 2, N_BLOCK]),
-                    in1=shift[:, :, n_cols],
-                    op=ALU.subtract,
-                )
+            def shift_state(j, banks):
+                nc.scalar.activation(out=shift[:, j, 0, :], in_=banks[0][:], func=ACT.Copy)
+                nc.scalar.activation(out=shift[:, j, 1, :], in_=banks[1][:], func=ACT.Exp)
+                for m in range(ROW_TILES):
+                    nc.gpsimd.tensor_tensor(
+                        out=uw[:, j, m],
+                        in0=sp_sb[:, j, m, :].unsqueeze(1).to_broadcast([P, 2, N_BLOCK]),
+                        in1=shift[:, j],
+                        op=ALU.subtract,
+                    )
+
+            turned_tiles = {0: turn(0), 1: turn(1)}
+            grouped_tiles = {}
+            for g in range(PASSES):
+                banks = spread(g)
+                planes = mix_pass(g, turned_tiles[g][0], turned_tiles[g][1])
+                shift_state(g, banks)
+                if g + 2 < PASSES:
+                    turned_tiles[g + 2] = turn(g + 2)
+                grouped_tiles[g] = regroup(planes)
+                if g >= 1:
+                    quantise(g - 1, grouped_tiles[g - 1])
+            quantise(PASSES - 1, grouped_tiles[PASSES - 1])
 
         with tc.tile_pool(name="work", bufs=3, reuse_waits="tile") as work, tc.psum_pool(
             name="staged", bufs=3, reuse_waits="tile"
         ) as staged:
-            for j in range(N_BLOCKS):
-                n_cols = slice(N_BLOCK * j, N_BLOCK * (j + 1))
-                for m in range(ROW_TILES):
-                    rows = slice(P * m, P * (m + 1))
-                    k_ps = sums.tile([P, N_BLOCK], F32)
-                    v_ps = sums.tile([P, N_BLOCK], F32)
-                    for s, product in enumerate((k_ps, v_ps)):
-                        for g in range(PASSES):
-                            nc.tensor.matmul_mx(
-                                out=product[:],
-                                lhsT=x_codes[:, g, s, rows].bitcast(FP8X4),
-                                lhsT_scale=x_scales[:, g, s, rows],
-                                rhs=w_words[:, s, g, n_cols].bitcast(FP8X4),
-                                rhs_scale=w_scales[4 * g : P, s, n_cols],
-                                start=(g == 0),
-                                stop=(g == PASSES - 1),
-                            )
-                    ab_ps = staged.tile([P, 2, N_BLOCK], BF16)
-                    for s in range(2):
-                        nc.tensor.matmul(
-                            out=ab_ps[:, s, :], lhsT=ident[:], rhs=ab_sb[:, s, m, n_cols], start=True, stop=True
-                        )
 
-                    first = work.tile([P, 2, N_BLOCK], F32)
-                    nc.vector.tensor_tensor(
-                        out=first[:],
-                        in0=uw[:, m, :, n_cols],
-                        in1=k_ps[:].unsqueeze(1).to_broadcast([P, 2, N_BLOCK]),
-                        op=ALU.subtract,
-                    )
-                    new_p = work.tile([P, N_BLOCK], F32)
-                    nc.vector.tensor_tensor(out=new_p[:], in0=uw[:, m, 1, n_cols], in1=k_ps[:], op=ALU.max)
-                    nc.sync.dma_start(out=out_4[rows, n_cols], in_=new_p[:])
-
-                    second = work.tile([P, 2, 2, N_BLOCK], F32)
-                    nc.scalar.activation(out=second[:, :, 1, :], in_=first[:], func=ACT.Relu)
-                    nc.scalar.activation(out=first[:], in_=first[:], func=ACT.Exp)
-                    nc.scalar.activation(out=second[:, :, 1, :], in_=second[:, :, 1, :], func=ACT.Exp, scale=-1.0)
-                    nc.vector.tensor_tensor(
-                        out=second[:, :, 0, :],
-                        in0=second[:, :, 1, :],
-                        in1=v_ps[:].unsqueeze(1).to_broadcast([P, 2, N_BLOCK]),
-                        op=ALU.mult,
-                    )
-                    result = work.tile([P, 2, 2, N_BLOCK], F32)
-                    for h, (out_a, out_b) in enumerate(((out_0, out_1), (out_2, out_3))):
-                        nc.vector.scalar_tensor_tensor(
-                            out=result[:, h],
-                            in0=first[:, h, :].unsqueeze(1).to_broadcast([P, 2, N_BLOCK]),
-                            scalar=1.0,
-                            in1=ab_ps[:],
-                            op0=ALU.min,
-                            op1=ALU.mult,
+            def project(i):
+                j, m = divmod(i, ROW_TILES)
+                rows = slice(P * m, P * (m + 1))
+                k_ps = sums.tile([P, N_BLOCK], F32)
+                v_ps = sums.tile([P, N_BLOCK], F32)
+                for s, product in enumerate((k_ps, v_ps)):
+                    for g in range(PASSES):
+                        nc.tensor.matmul_mx(
+                            out=product[:],
+                            lhsT=x_codes[:, g, s, rows].bitcast(FP8X4),
+                            lhsT_scale=x_scales[:, g, s, rows],
+                            rhs=w_words[:, j, s, g, :].bitcast(FP8X4),
+                            rhs_scale=w_scales[4 * g : P, s, n_cols(j)],
+                            start=(g == 0),
+                            stop=(g == PASSES - 1),
                         )
-                        nc.gpsimd.tensor_tensor(out=result[:, h], in0=result[:, h], in1=second[:, h], op=ALU.add)
-                        nc.sync.dma_start(out=out_a[rows, n_cols], in_=result[:, h, 0, :])
-                        nc.sync.dma_start(out=out_b[rows, n_cols], in_=result[:, h, 1, :])
+                ab_ps = staged.tile([P, 2, N_BLOCK], BF16)
+                for s in range(2):
+                    nc.tensor.matmul(
+                        out=ab_ps[:, s, :], lhsT=ident[:], rhs=ab_sb[:, j, s, m, :], start=True, stop=True
+                    )
+                return k_ps, v_ps, ab_ps
+
+
+            def exponents(i, k_ps):
+                j, m = divmod(i, ROW_TILES)
+                first = work.tile([P, 2, N_BLOCK], F32)
+                nc.vector.tensor_tensor(
+                    out=first[:],
+                    in0=uw[:, j, m],
+                    in1=k_ps[:].unsqueeze(1).to_broadcast([P, 2, N_BLOCK]),
+                    op=ALU.subtract,
+                )
+                new_p = work.tile([P, N_BLOCK], F32)
+                nc.vector.tensor_tensor(out=new_p[:], in0=uw[:, j, m, 1, :], in1=k_ps[:], op=ALU.max)
+                nc.sync.dma_start(out=out_4[P * m : P * (m + 1), n_cols(j)], in_=new_p[:])
+                second = work.tile([P, 2, 2, N_BLOCK], F32)
+                nc.scalar.activation(out=second[:, :, 1, :], in_=first[:], func=ACT.Relu)
+                nc.scalar.activation(out=second[:, :, 1, :], in_=second[:, :, 1, :], func=ACT.Exp, scale=-1.0)
+                nc.scalar.activation(out=first[:], in_=first[:], func=ACT.Exp)
+                return first, second
+
+            def combine(i, first, second, v_ps, ab_ps):
+                j, m = divmod(i, ROW_TILES)
+                rows = slice(P * m, P * (m + 1))
+                nc.vector.tensor_tensor(
+                    out=second[:, :, 0, :],
+                    in0=second[:, :, 1, :],
+                    in1=v_ps[:].unsqueeze(1).to_broadcast([P, 2, N_BLOCK]),
+                    op=ALU.mult,
+                )
+                result = work.tile([P, 2, 2, N_BLOCK], F32)
+                for h, (out_a, out_b) in enumerate(((out_0, out_1), (out_2, out_3))):
+                    nc.vector.scalar_tensor_tensor(
+                        out=result[:, h],
+                        in0=first[:, h, :].unsqueeze(1).to_broadcast([P, 2, N_BLOCK]),
+                        scalar=1.0,
+                        in1=ab_ps[:],
+                        op0=ALU.min,
+                        op1=ALU.mult,
+                    )
+                    nc.gpsimd.tensor_tensor(out=result[:, h], in0=result[:, h], in1=second[:, h], op=ALU.add)
+                    nc.sync.dma_start(out=out_a[rows, n_cols(j)], in_=result[:, h, 0, :])
+                    nc.sync.dma_start(out=out_b[rows, n_cols(j)], in_=result[:, h, 1, :])
+
+            banks_of = {0: project(0), 1: project(1)}
+            exps_of = {0: exponents(0, banks_of[0][0])}
+            for i in range(UNITS):
+                if i + 1 < UNITS:
+                    exps_of[i + 1] = exponents(i + 1, banks_of[i + 1][0])
+                combine(i, exps_of[i][0], exps_of[i][1], banks_of[i][1], banks_of[i][2])
+                if i + 2 < UNITS:
+                    banks_of[i + 2] = project(i + 2)

@@ -22,6 +22,7 @@ N_BLOCK = 512
 N_BLOCKS = D // N_BLOCK
 UNITS = N_BLOCKS * ROW_TILES
 QUADRANTS = 4
+VECTOR_SUMS = 1
 
 FLOPS = 2 * 2 * B * E * D
 
@@ -57,10 +58,12 @@ def tile_rwkv_timemix_for_quant_pa_kernel(
     with tc.manual_schedule(), tc.tile_pool(name="keep", bufs=1) as keep, tc.psum_pool(name="sums", bufs=2) as sums:
         ident = keep.tile([P, P], BF16)
         make_identity(nc, ident[:])
+        warm = keep.tile([P, 1], F32)
+        nc.vector.memset(warm[:], 0.0)
+        nc.scalar.activation(out=warm[:], in_=warm[:], func=ACT.Exp)
 
         w_words = keep.tile([P, N_BLOCKS, 2, PASSES, N_BLOCK], U32, align_bytes=64)
         w_scales = keep.tile([P, 2, D], U8, align_bytes=64)
-        nc.vector.memset(w_scales[:].bitcast(I32), 0)
         x_codes = keep.tile([P, PASSES, 2, B], U32, align_bytes=64)
         x_scales = keep.tile([P, PASSES, 2, B], U8, align_bytes=64)
         ab_sb = keep.tile([P, N_BLOCKS, 2, ROW_TILES, N_BLOCK], BF16)
@@ -80,6 +83,7 @@ def tile_rwkv_timemix_for_quant_pa_kernel(
             nc.vector.memset(lone_rows[:].bitcast(I32), 0)
             ones = inputs.tile([P, P], BF16)
             nc.vector.memset(ones[:], 1.0)
+            nc.vector.memset(w_scales[:].bitcast(I32), 0)
 
             by_row_tile = "(m p) c -> p m c"
             for g in range(PASSES):
@@ -189,14 +193,14 @@ def tile_rwkv_timemix_for_quant_pa_kernel(
                         op=ALU.subtract,
                     )
 
-            turned_tiles = {0: turn(0), 1: turn(1)}
+            turned_tiles = {0: turn(0)}
             grouped_tiles = {}
             for g in range(PASSES):
                 banks = spread(g)
+                if g + 1 < PASSES:
+                    turned_tiles[g + 1] = turn(g + 1)
                 planes = mix_pass(g, turned_tiles[g][0], turned_tiles[g][1])
                 shift_state(g, banks)
-                if g + 2 < PASSES:
-                    turned_tiles[g + 2] = turn(g + 2)
                 grouped_tiles[g] = regroup(planes)
                 if g >= 1:
                     quantise(g - 1, grouped_tiles[g - 1])
@@ -249,6 +253,7 @@ def tile_rwkv_timemix_for_quant_pa_kernel(
                 return first, second
 
             def combine(i, first, second, v_ps, ab_ps):
+                adder = nc.gpsimd if i < UNITS - VECTOR_SUMS else nc.vector
                 j, m = divmod(i, ROW_TILES)
                 rows = slice(P * m, P * (m + 1))
                 nc.vector.tensor_tensor(
@@ -267,7 +272,7 @@ def tile_rwkv_timemix_for_quant_pa_kernel(
                         op0=ALU.min,
                         op1=ALU.mult,
                     )
-                    nc.gpsimd.tensor_tensor(out=result[:, h], in0=result[:, h], in1=second[:, h], op=ALU.add)
+                    adder.tensor_tensor(out=result[:, h], in0=result[:, h], in1=second[:, h], op=ALU.add)
                     nc.sync.dma_start(out=out_a[rows, n_cols(j)], in_=result[:, h, 0, :])
                     nc.sync.dma_start(out=out_b[rows, n_cols(j)], in_=result[:, h, 1, :])
 

@@ -22,7 +22,6 @@ N_BLOCK = 512
 N_BLOCKS = D // N_BLOCK
 UNITS = N_BLOCKS * ROW_TILES
 QUADRANTS = 4
-VECTOR_SUMS = 1
 
 FLOPS = 2 * 2 * B * E * D
 
@@ -210,28 +209,33 @@ def tile_rwkv_timemix_for_quant_pa_kernel(
             name="staged", bufs=3, reuse_waits="tile"
         ) as staged:
 
-            def project(i):
+            def product_of(i, s):
                 j, m = divmod(i, ROW_TILES)
                 rows = slice(P * m, P * (m + 1))
-                k_ps = sums.tile([P, N_BLOCK], F32)
-                v_ps = sums.tile([P, N_BLOCK], F32)
-                for s, product in enumerate((k_ps, v_ps)):
-                    for g in range(PASSES):
-                        nc.tensor.matmul_mx(
-                            out=product[:],
-                            lhsT=x_codes[:, g, s, rows].bitcast(FP8X4),
-                            lhsT_scale=x_scales[:, g, s, rows],
-                            rhs=w_words[:, j, s, g, :].bitcast(FP8X4),
-                            rhs_scale=w_scales[4 * g : P, s, n_cols(j)],
-                            start=(g == 0),
-                            stop=(g == PASSES - 1),
-                        )
+                product = sums.tile([P, N_BLOCK], F32, tag=("k_ps", "v_ps")[s])
+                for g in range(PASSES):
+                    nc.tensor.matmul_mx(
+                        out=product[:],
+                        lhsT=x_codes[:, g, s, rows].bitcast(FP8X4),
+                        lhsT_scale=x_scales[:, g, s, rows],
+                        rhs=w_words[:, j, s, g, :].bitcast(FP8X4),
+                        rhs_scale=w_scales[4 * g : P, s, n_cols(j)],
+                        start=(g == 0),
+                        stop=(g == PASSES - 1),
+                    )
+                return product
+
+            def stage_states(i):
+                j, m = divmod(i, ROW_TILES)
                 ab_ps = staged.tile([P, 2, N_BLOCK], BF16)
                 for s in range(2):
                     nc.tensor.matmul(
                         out=ab_ps[:, s, :], lhsT=ident[:], rhs=ab_sb[:, j, s, m, :], start=True, stop=True
                     )
-                return k_ps, v_ps, ab_ps
+                return ab_ps
+
+            def project(i):
+                return product_of(i, 0), product_of(i, 1), stage_states(i)
 
 
             def exponents(i, k_ps):
@@ -253,7 +257,6 @@ def tile_rwkv_timemix_for_quant_pa_kernel(
                 return first, second
 
             def combine(i, first, second, v_ps, ab_ps):
-                adder = nc.gpsimd if i < UNITS - VECTOR_SUMS else nc.vector
                 j, m = divmod(i, ROW_TILES)
                 rows = slice(P * m, P * (m + 1))
                 nc.vector.tensor_tensor(
@@ -272,11 +275,13 @@ def tile_rwkv_timemix_for_quant_pa_kernel(
                         op0=ALU.min,
                         op1=ALU.mult,
                     )
+                    adder = nc.vector if i == UNITS - 1 else nc.gpsimd
                     adder.tensor_tensor(out=result[:, h], in0=result[:, h], in1=second[:, h], op=ALU.add)
                     nc.sync.dma_start(out=out_a[rows, n_cols(j)], in_=result[:, h, 0, :])
                     nc.sync.dma_start(out=out_b[rows, n_cols(j)], in_=result[:, h, 1, :])
 
-            banks_of = {0: project(0), 1: project(1)}
+            first_k = [product_of(0, 0), product_of(1, 0)]
+            banks_of = {i: (first_k[i], product_of(i, 1), stage_states(i)) for i in range(2)}
             exps_of = {0: exponents(0, banks_of[0][0])}
             for i in range(UNITS):
                 if i + 1 < UNITS:

@@ -21,6 +21,7 @@ ROW_TILES = B // P
 N_BLOCK = 512
 N_BLOCKS = D // N_BLOCK
 UNITS = N_BLOCKS * ROW_TILES
+HALVES = 2
 QUADRANTS = 4
 
 FLOPS = 2 * 2 * B * E * D
@@ -57,6 +58,8 @@ def tile_rwkv_timemix_for_quant_pa_kernel(
     with tc.manual_schedule(), tc.tile_pool(name="keep", bufs=1) as keep, tc.psum_pool(name="sums", bufs=2) as sums:
         ident = keep.tile([P, P], BF16)
         make_identity(nc, ident[:])
+        ident_words = keep.tile([P, P], F32)
+        make_identity(nc, ident_words[:])
         warm = keep.tile([P, 1], F32)
         nc.vector.memset(warm[:], 0.0)
         nc.scalar.activation(out=warm[:], in_=warm[:], func=ACT.Exp)
@@ -124,14 +127,20 @@ def tile_rwkv_timemix_for_quant_pa_kernel(
             )
 
             def turn(g):
-                x_turned = turned.tile([P, PACK, B], BF16)
-                sx_turned = turned.tile([P, PACK, B], BF16)
-                for t in range(PACK):
-                    for m in range(ROW_TILES):
-                        rows = slice(P * m, P * (m + 1))
-                        nc.tensor.transpose(x_turned[:, t, rows], x_sb[:, g, m, t:K_PASS:PACK], ident[:])
-                        nc.tensor.transpose(sx_turned[:, t, rows], sx_sb[:, g, m, t:K_PASS:PACK], ident[:])
-                return x_turned, sx_turned
+                views = []
+                for source, tag in ((sx_sb, "sx_turned"), (x_sb, "x_turned")):
+                    words = turned.tile([P, HALVES, B], F32, tag=tag)
+                    for h in range(HALVES):
+                        for m in range(ROW_TILES):
+                            nc.tensor.transpose(
+                                words[:, h, P * m : P * (m + 1)],
+                                source[:, g, m, :].bitcast(F32)[:, h : K_PASS // 2 : HALVES],
+                                ident_words[:],
+                            )
+                    views.append(
+                        words[:].rearrange("p h b -> p (h b)").bitcast(BF16).rearrange("p (h b e) -> p h b e", h=HALVES, e=2)
+                    )
+                return views[1], views[0]
 
             def mix_pass(g, x_turned, sx_turned):
                 sx_share = mixing.tile([P, 2, PACK, B], F32)
@@ -141,13 +150,13 @@ def tile_rwkv_timemix_for_quant_pa_kernel(
                         col = PACK * g + t
                         nc.scalar.activation(
                             out=sx_share[:, s, t, :],
-                            in_=sx_turned[:, t, :],
+                            in_=sx_turned[:, t // 2, :, t % 2],
                             func=ACT.Copy,
                             scale=rest[:, s, col : col + 1],
                         )
                         nc.vector.scalar_tensor_tensor(
                             out=planes[:, s, t, :],
-                            in0=x_turned[:, t, :],
+                            in0=x_turned[:, t // 2, :, t % 2],
                             scalar=mix[:, s, col : col + 1],
                             in1=sx_share[:, s, t, :],
                             op0=ALU.mult,

@@ -22,6 +22,8 @@ N_BLOCK = 512
 N_BLOCKS = D // N_BLOCK
 UNITS = N_BLOCKS * ROW_TILES
 HALVES = 2
+STORE_BUFS_P = 6
+STORE_BUFS_AB = 4
 QUADRANTS = 4
 
 FLOPS = 2 * 2 * B * E * D
@@ -256,7 +258,7 @@ def tile_rwkv_timemix_for_quant_pa_kernel(
                     in1=k_ps[:].unsqueeze(1).to_broadcast([P, 2, N_BLOCK]),
                     op=ALU.subtract,
                 )
-                new_p = work.tile([P, N_BLOCK], F32)
+                new_p = work.tile([P, N_BLOCK], F32, bufs=STORE_BUFS_P)
                 nc.vector.tensor_tensor(out=new_p[:], in0=uw[:, j, m, 1, :], in1=k_ps[:], op=ALU.max)
                 nc.sync.dma_start(out=out_4[P * m : P * (m + 1), n_cols(j)], in_=new_p[:])
                 second = work.tile([P, 2, 2, N_BLOCK], F32)
@@ -274,7 +276,7 @@ def tile_rwkv_timemix_for_quant_pa_kernel(
                     in1=v_ps[:].unsqueeze(1).to_broadcast([P, 2, N_BLOCK]),
                     op=ALU.mult,
                 )
-                result = work.tile([P, 2, 2, N_BLOCK], F32)
+                result = work.tile([P, 2, 2, N_BLOCK], F32, bufs=STORE_BUFS_AB)
                 for h, (out_a, out_b) in enumerate(((out_0, out_1), (out_2, out_3))):
                     nc.vector.scalar_tensor_tensor(
                         out=result[:, h],

@@ -24,6 +24,7 @@ UNITS = N_BLOCKS * ROW_TILES
 HALVES = 2
 STORE_BUFS_P = 6
 STORE_BUFS_AB = 4
+VECTOR_SUMS = 3
 QUADRANTS = 4
 
 FLOPS = 2 * 2 * B * E * D
@@ -277,7 +278,7 @@ def tile_rwkv_timemix_for_quant_pa_kernel(
                     op=ALU.mult,
                 )
                 result = work.tile([P, 2, 2, N_BLOCK], F32, bufs=STORE_BUFS_AB)
-                for h, (out_a, out_b) in enumerate(((out_0, out_1), (out_2, out_3))):
+                for h in range(2):
                     nc.vector.scalar_tensor_tensor(
                         out=result[:, h],
                         in0=first[:, h, :].unsqueeze(1).to_broadcast([P, 2, N_BLOCK]),
@@ -286,11 +287,20 @@ def tile_rwkv_timemix_for_quant_pa_kernel(
                         op0=ALU.min,
                         op1=ALU.mult,
                     )
-                    adder = nc.vector if i == UNITS - 1 else nc.gpsimd
-                    adder.tensor_tensor(out=result[:, h], in0=result[:, h], in1=second[:, h], op=ALU.add)
-                    nc.sync.dma_start(out=out_a[rows, n_cols(j)], in_=result[:, h, 0, :])
-                    nc.sync.dma_start(out=out_b[rows, n_cols(j)], in_=result[:, h, 1, :])
+                    if 2 * i + h < 2 * UNITS - VECTOR_SUMS:
+                        add_and_store(nc.gpsimd, i, h, result, second)
+                    else:
+                        late_sums.append((i, h, result, second))
 
+            def add_and_store(adder, i, h, result, second):
+                j, m = divmod(i, ROW_TILES)
+                rows = slice(P * m, P * (m + 1))
+                out_a, out_b = ((out_0, out_1), (out_2, out_3))[h]
+                adder.tensor_tensor(out=result[:, h], in0=result[:, h], in1=second[:, h], op=ALU.add)
+                nc.sync.dma_start(out=out_a[rows, n_cols(j)], in_=result[:, h, 0, :])
+                nc.sync.dma_start(out=out_b[rows, n_cols(j)], in_=result[:, h, 1, :])
+
+            late_sums = []
             first_k = [product_of(0, 0), product_of(1, 0)]
             banks_of = {i: (first_k[i], product_of(i, 1), stage_states(i)) for i in range(2)}
             exps_of = {0: exponents(0, banks_of[0][0])}
@@ -300,3 +310,5 @@ def tile_rwkv_timemix_for_quant_pa_kernel(
                 combine(i, exps_of[i][0], exps_of[i][1], banks_of[i][1], banks_of[i][2])
                 if i + 2 < UNITS:
                     banks_of[i + 2] = project(i + 2)
+            for i, h, result, second in late_sums:
+                add_and_store(nc.vector, i, h, result, second)

@@ -21,9 +21,10 @@ ROW_TILES = B // P
 N_BLOCK = 512
 N_BLOCKS = D // N_BLOCK
 UNITS = N_BLOCKS * ROW_TILES
+C_TILES = N_BLOCK // P
 HALVES = 2
-STORE_BUFS_P = 6
-STORE_BUFS_AB = 4
+STORE_BUFS_P = 5
+STORE_BUFS_AB = 5
 VECTOR_SUMS = 3
 QUADRANTS = 4
 
@@ -53,12 +54,11 @@ def tile_rwkv_timemix_for_quant_pa_kernel(
 ):
     nc = tc.nc
     weights = ((W_key_words, W_key_scales), (W_value_words, W_value_scales))
-    assert N_BLOCKS == PASSES
 
     def n_cols(j):
         return slice(N_BLOCK * j, N_BLOCK * (j + 1))
 
-    with tc.manual_schedule(), tc.tile_pool(name="keep", bufs=1) as keep, tc.psum_pool(name="sums", bufs=2) as sums:
+    with tc.manual_schedule(), tc.tile_pool(name="keep", bufs=1) as keep, tc.psum_pool(name="banks", bufs=1) as banks:
         ident = keep.tile([P, P], BF16)
         make_identity(nc, ident[:])
         ident_words = keep.tile([P, P], F32)
@@ -73,21 +73,26 @@ def tile_rwkv_timemix_for_quant_pa_kernel(
         x_scales = keep.tile([P, PASSES, 2, B], U8, align_bytes=64)
         ab_sb = keep.tile([P, N_BLOCKS, 2, ROW_TILES, N_BLOCK], BF16)
         sp_sb = keep.tile([P, N_BLOCKS, ROW_TILES, N_BLOCK], BF16)
-        shift = keep.tile([P, N_BLOCKS, 2, N_BLOCK], F32)
-        uw = keep.tile([P, N_BLOCKS, ROW_TILES, 2, N_BLOCK], F32)
+        sp_turned = keep.tile([P, 2, C_TILES, B], BF16)
+        neg_shift = keep.tile([P, 2, D // P], F32)
         mix_bf = keep.tile([P, 2, PASSES, PACK], BF16)
         mix = keep.tile([P, 2, PASSES * PACK], F32)
         rest = keep.tile([P, 2, PASSES * PACK], F32)
+        shift_rows = keep.tile([P, P], BF16)
 
-        with tc.tile_pool(name="inputs", bufs=1) as inputs, tc.tile_pool(
-            name="mixing", bufs=2
-        ) as mixing, tc.psum_pool(name="turned", bufs=2) as turned:
+        def turn_states(j):
+            turned_ps = banks.tile([P, C_TILES, B], BF16, tag=("kb", "ka", "ka", "ka")[j])
+            for c in range(C_TILES):
+                for m in range(ROW_TILES):
+                    nc.tensor.transpose(
+                        turned_ps[:, c, P * m : P * (m + 1)], sp_sb[:, j, m, P * c : P * (c + 1)], ident[:]
+                    )
+            nc.scalar.copy(out=sp_turned[:, j % 2], in_=turned_ps[:])
+
+        with tc.tile_pool(name="inputs", bufs=1) as inputs, tc.tile_pool(name="mixing", bufs=4) as mixing:
             x_sb = inputs.tile([P, PASSES, ROW_TILES, K_PASS], BF16)
             sx_sb = inputs.tile([P, PASSES, ROW_TILES, K_PASS], BF16)
-            lone_rows = inputs.tile([P, 2, D], BF16)
-            nc.vector.memset(lone_rows[:].bitcast(I32), 0)
-            ones = inputs.tile([P, P], BF16)
-            nc.vector.memset(ones[:], 1.0)
+            nc.vector.memset(shift_rows[:].bitcast(I32), 0)
             nc.vector.memset(w_scales[:].bitcast(I32), 0)
 
             by_row_tile = "(m p) c -> p m c"
@@ -101,23 +106,42 @@ def tile_rwkv_timemix_for_quant_pa_kernel(
                             out=mix_bf[:, s], in_=time_mix[0].rearrange("(g p t) -> p g t", g=PASSES, p=P)
                         )
                     for s, vector in enumerate((time_first, time_decay)):
-                        nc.sync.dma_start(out=lone_rows[0:1, s, :], in_=vector.unsqueeze(0))
-                nc.sync.dma_start(out=sp_sb[:, g], in_=state_p.rearrange(by_row_tile, p=P)[:, :, n_cols(g)])
-            for s in range(2):
+                        nc.sync.dma_start(
+                            out=shift_rows[16 * s : 16 * (s + 1), :], in_=vector.rearrange("(c p) -> c p", p=P)
+                        )
+            def load_p(j):
+                nc.sync.dma_start(out=sp_sb[:, j], in_=state_p.rearrange(by_row_tile, p=P)[:, :, n_cols(j)])
+
+            def load_scales(s):
                 for quad in range(QUADRANTS):
                     nc.sync.dma_start(
                         out=w_scales[32 * quad : 32 * quad + 16, s, :].bitcast(I32),
                         in_=weights[s][1][:, 4 * quad : 4 * quad + 4, :].bitcast(I32),
                     )
-            for j in range(N_BLOCKS):
-                for s in range(2):
-                    words = weights[s][0].rearrange("g p n t -> p g (n t)")
-                    nc.sync.dma_start(
-                        out=w_words[:, j, s].bitcast(I32),
-                        in_=words[:, :, PACK * N_BLOCK * j : PACK * N_BLOCK * (j + 1)].bitcast(I32),
-                    )
+
+            def load_words(j, s):
+                words = weights[s][0].rearrange("g p n t -> p g (n t)")
+                nc.sync.dma_start(
+                    out=w_words[:, j, s].bitcast(I32),
+                    in_=words[:, :, PACK * N_BLOCK * j : PACK * N_BLOCK * (j + 1)].bitcast(I32),
+                )
+
+            def load_ab(j):
                 for s, state in enumerate((state_A, state_B)):
                     nc.sync.dma_start(out=ab_sb[:, j, s], in_=state.rearrange(by_row_tile, p=P)[:, :, n_cols(j)])
+
+            load_p(0)
+            load_p(1)
+            load_scales(0)
+            load_words(0, 0)
+            load_scales(1)
+            load_words(1, 0)
+            for j in range(N_BLOCKS):
+                load_words(j, 1)
+                load_ab(j)
+                if j + 2 < N_BLOCKS:
+                    load_p(j + 2)
+                    load_words(j + 2, 0)
 
             nc.vector.tensor_copy(out=mix[:], in_=mix_bf[:].rearrange("p s g t -> p s (g t)"))
             nc.vector.tensor_scalar(
@@ -130,9 +154,10 @@ def tile_rwkv_timemix_for_quant_pa_kernel(
             )
 
             def turn(g):
+                tags = (("p", "s"), ("e0", "e1"), ("v", "ab"), ("p", "s"))
                 views = []
-                for source, tag in ((sx_sb, "sx_turned"), (x_sb, "x_turned")):
-                    words = turned.tile([P, HALVES, B], F32, tag=tag)
+                for k, source in enumerate((sx_sb, x_sb)):
+                    words = banks.tile([P, HALVES, B], F32, tag=tags[g][k])
                     for h in range(HALVES):
                         for m in range(ROW_TILES):
                             nc.tensor.transpose(
@@ -145,132 +170,200 @@ def tile_rwkv_timemix_for_quant_pa_kernel(
                     )
                 return views[1], views[0]
 
-            def mix_pass(g, x_turned, sx_turned):
-                sx_share = mixing.tile([P, 2, PACK, B], F32)
-                planes = mixing.tile([P, 2, PACK, B], BF16)
-                for s in range(2):
-                    for t in range(PACK):
-                        col = PACK * g + t
-                        nc.scalar.activation(
-                            out=sx_share[:, s, t, :],
-                            in_=sx_turned[:, t // 2, :, t % 2],
-                            func=ACT.Copy,
-                            scale=rest[:, s, col : col + 1],
-                        )
-                        nc.vector.scalar_tensor_tensor(
-                            out=planes[:, s, t, :],
-                            in0=x_turned[:, t // 2, :, t % 2],
-                            scalar=mix[:, s, col : col + 1],
-                            in1=sx_share[:, s, t, :],
-                            op0=ALU.mult,
-                            op1=ALU.add,
-                        )
-                return planes
+            def mix_half(g, s, planes):
+                x_turned, sx_turned = turned_tiles[g]
+                sx_share = mixing.tile([P, PACK, B], F32, bufs=4)
+                for t in range(PACK):
+                    col = PACK * g + t
+                    nc.scalar.activation(
+                        out=sx_share[:, t, :],
+                        in_=sx_turned[:, t // 2, :, t % 2],
+                        func=ACT.Copy,
+                        scale=rest[:, s, col : col + 1],
+                    )
+                    nc.vector.scalar_tensor_tensor(
+                        out=planes[:, s, t, :],
+                        in0=x_turned[:, t // 2, :, t % 2],
+                        scalar=mix[:, s, col : col + 1],
+                        in1=sx_share[:, t, :],
+                        op0=ALU.mult,
+                        op1=ALU.add,
+                    )
 
-            def regroup(planes):
-                grouped = mixing.tile([P, 2, B, PACK], BF16, align_bytes=64)
-                for s in range(2):
+            def regroup(planes, grouped, s, engine):
+                if engine == 0:
+                    nc.gpsimd.tensor_scalar(
+                        out=grouped[:, s],
+                        in0=planes[:, s].rearrange("p t b -> p b t"),
+                        scalar1=1.0,
+                        scalar2=0.0,
+                        op0=ALU.mult,
+                        op1=ALU.add,
+                    )
+                else:
                     nc.vector.tensor_copy(
                         out=grouped[:, s].rearrange("p (c i) t -> p c t i", i=4),
                         in_=planes[:, s].rearrange("p t (c i) -> p c t i", i=4),
                     )
-                return grouped
 
-            def quantise(g, grouped):
+            def quantise(g, grouped, first_s, last_s):
                 nc.vector.quantize_mx(
-                    out=x_codes[:, g].rearrange("p s b -> p (s b)").bitcast(FP8X4),
-                    scales=x_scales[:, g].rearrange("p s b -> p (s b)"),
-                    in_=grouped[:].rearrange("p s b t -> p (s b t)"),
+                    out=x_codes[:, g, first_s : last_s + 1].rearrange("p s b -> p (s b)").bitcast(FP8X4),
+                    scales=x_scales[:, g, first_s : last_s + 1].rearrange("p s b -> p (s b)"),
+                    in_=grouped[:, first_s : last_s + 1].rearrange("p s b t -> p (s b t)"),
                 )
 
-            def spread(j):
-                banks = []
-                for s in range(2):
-                    spread_ps = sums.tile([P, N_BLOCK], F32, tag=("k_ps", "v_ps")[s])
-                    nc.tensor.matmul(
-                        out=spread_ps[:], lhsT=ones[:], rhs=lone_rows[:, s, n_cols(j)], start=True, stop=True
-                    )
-                    banks.append(spread_ps)
-                return banks
+            turned_tiles = {0: turn(0)}
+            planes_of, grouped_of = {}, {}
+            shift_ps = banks.tile([P, P], BF16, tag="ka")
+            nc.tensor.transpose(shift_ps[:], shift_rows[:], ident[:])
 
-            def shift_state(j, banks):
-                nc.scalar.activation(out=shift[:, j, 0, :], in_=banks[0][:], func=ACT.Copy)
-                nc.scalar.activation(out=shift[:, j, 1, :], in_=banks[1][:], func=ACT.Exp)
-                for m in range(ROW_TILES):
-                    nc.gpsimd.tensor_tensor(
-                        out=uw[:, j, m],
-                        in0=sp_sb[:, j, m, :].unsqueeze(1).to_broadcast([P, 2, N_BLOCK]),
-                        in1=shift[:, j],
+            def open_round(g):
+                planes = mixing.tile([P, 2, PACK, B], BF16)
+                grouped = mixing.tile([P, 2, B, PACK], BF16, align_bytes=64)
+                planes_of[g], grouped_of[g] = planes, grouped
+
+            turned_tiles[1] = turn(1)
+            turned_tiles[2] = turn(2)
+            for g in range(PASSES):
+                open_round(g)
+            mix_half(0, 0, planes_of[0])
+            regroup(planes_of[0], grouped_of[0], 0, 0)
+            mix_half(0, 1, planes_of[0])
+            regroup(planes_of[0], grouped_of[0], 1, 0)
+            spread = shift_ps[:, 0:32].rearrange("p (h c) -> p h c", h=2)
+            decay = keep.tile([P, D // P], F32)
+            nc.scalar.activation(out=decay[:], in_=spread[:, 1], func=ACT.Exp)
+            nc.vector.tensor_scalar_mul(neg_shift[:, 0], spread[:, 0], -1.0)
+            nc.vector.tensor_scalar_mul(neg_shift[:, 1], decay[:], -1.0)
+            turned_tiles[3] = turn(3)
+            mix_half(1, 0, planes_of[1])
+            regroup(planes_of[1], grouped_of[1], 0, 0)
+            quantise(0, grouped_of[0], 0, 1)
+            mix_half(2, 0, planes_of[2])
+            regroup(planes_of[2], grouped_of[2], 0, 0)
+            quantise(1, grouped_of[1], 0, 0)
+            mix_half(3, 0, planes_of[3])
+            turn_states(0)
+            regroup(planes_of[3], grouped_of[3], 0, 1)
+            quantise(2, grouped_of[2], 0, 0)
+            quantise(3, grouped_of[3], 0, 0)
+
+            def keys_of(j):
+                pair = []
+                for half in range(2):
+                    k_ps = banks.tile([P, 2, B], F32, tag=("ka", "kb")[half])
+                    for e in range(2):
+                        c = 2 * half + e
+                        for g in range(PASSES):
+                            nc.tensor.matmul_mx(
+                                out=k_ps[:, e, :],
+                                lhsT=w_words[:, j, 0, g, P * c : P * (c + 1)].bitcast(FP8X4),
+                                lhsT_scale=w_scales[4 * g : P, 0, N_BLOCK * j + P * c : N_BLOCK * j + P * (c + 1)],
+                                rhs=x_codes[:, g, 0, :].bitcast(FP8X4),
+                                rhs_scale=x_scales[:, g, 0, :],
+                                start=(g == 0),
+                                stop=(g == PASSES - 1),
+                            )
+                    pair.append(k_ps)
+                return pair
+
+            def split(j, keys):
+                z = keep.tile([P, C_TILES, B], F32, bufs=2)
+                new_p = keep.tile([P, C_TILES, B], F32, bufs=2)
+                for half in range(2):
+                    nc.vector.tensor_tensor(
+                        out=z[:, 2 * half : 2 * half + 2],
+                        in0=sp_turned[:, j % 2, 2 * half : 2 * half + 2],
+                        in1=keys[half][:],
                         op=ALU.subtract,
                     )
+                for c in range(C_TILES):
+                    ch = C_TILES * j + c
+                    nc.vector.scalar_tensor_tensor(
+                        out=new_p[:, c, :],
+                        in0=sp_turned[:, j % 2, c, :],
+                        scalar=neg_shift[:, 1, ch : ch + 1],
+                        in1=keys[c // 2][:, c % 2, :],
+                        op0=ALU.add,
+                        op1=ALU.max,
+                    )
+                return z, new_p
 
-            turned_tiles = {0: turn(0)}
-            grouped_tiles = {}
-            for g in range(PASSES):
-                banks = spread(g)
-                if g + 1 < PASSES:
-                    turned_tiles[g + 1] = turn(g + 1)
-                planes = mix_pass(g, turned_tiles[g][0], turned_tiles[g][1])
-                shift_state(g, banks)
-                grouped_tiles[g] = regroup(planes)
-                if g >= 1:
-                    quantise(g - 1, grouped_tiles[g - 1])
-            quantise(PASSES - 1, grouped_tiles[PASSES - 1])
 
-        with tc.tile_pool(name="work", bufs=3, reuse_waits="tile") as work, tc.psum_pool(
-            name="staged", bufs=3, reuse_waits="tile"
-        ) as staged:
-
-            def product_of(i, s):
+            def exponents(i, z, new_p):
                 j, m = divmod(i, ROW_TILES)
                 rows = slice(P * m, P * (m + 1))
-                product = sums.tile([P, N_BLOCK], F32, tag=("k_ps", "v_ps")[s])
+                first = keep.tile([P, 2, N_BLOCK], F32, bufs=3)
+                second = keep.tile([P, 2, 2, N_BLOCK], F32, bufs=3)
+                for h in range(2):
+                    e_ps = banks.tile([P, N_BLOCK], F32, tag=("e0", "e1")[h])
+                    for c in range(C_TILES):
+                        cols = slice(P * c, P * (c + 1))
+                        ch = C_TILES * j + c
+                        nc.tensor.matmul(
+                            out=e_ps[:, cols], lhsT=z[:, c, rows], rhs=ident_words[:],
+                            start=True, stop=False, is_transpose=True,
+                        )
+                        nc.tensor.matmul(
+                            out=e_ps[:, cols], lhsT=neg_shift[:, h, ch : ch + 1].to_broadcast([P, P]), rhs=ident_words[:],
+                            start=False, stop=True, is_transpose=True,
+                        )
+                    nc.scalar.activation(out=second[:, h, 1, :], in_=e_ps[:], func=ACT.Relu)
+                    nc.scalar.activation(out=first[:, h, :], in_=e_ps[:], func=ACT.Exp)
+                    nc.scalar.activation(out=second[:, h, 1, :], in_=second[:, h, 1, :], func=ACT.Exp, scale=-1.0)
+                p_ps = banks.tile([P, N_BLOCK], F32, tag="p")
+                for c in range(C_TILES):
+                    nc.tensor.transpose(p_ps[:, P * c : P * (c + 1)], new_p[:, c, rows], ident_words[:])
+                p_out = keep.tile([P, N_BLOCK], F32, bufs=STORE_BUFS_P)
+                nc.scalar.copy(out=p_out[:], in_=p_ps[:])
+                nc.sync.dma_start(out=out_4[rows, n_cols(j)], in_=p_out[:])
+                return first, second
+
+            mix_half(1, 1, planes_of[1])
+            regroup(planes_of[1], grouped_of[1], 1, 0)
+            turn_states(1)
+            keys = keys_of(0)
+            mix_half(3, 1, planes_of[3])
+            regroup(planes_of[3], grouped_of[3], 1, 0)
+            splits = {0: split(0, keys)}
+            mix_half(2, 1, planes_of[2])
+            exps = {0: exponents(0, splits[0][0], splits[0][1])}
+            keys = keys_of(1)
+            quantise(1, grouped_of[1], 1, 1)
+            regroup(planes_of[2], grouped_of[2], 1, 1)
+            quantise(3, grouped_of[3], 1, 1)
+            quantise(2, grouped_of[2], 1, 1)
+            splits[1] = split(1, keys)
+
+        with tc.tile_pool(name="work", bufs=3, reuse_waits="tile") as work:
+
+            def value_of(i):
+                j, m = divmod(i, ROW_TILES)
+                rows = slice(P * m, P * (m + 1))
+                v_ps = banks.tile([P, N_BLOCK], F32, tag=("v", "s")[i % 2])
                 for g in range(PASSES):
                     nc.tensor.matmul_mx(
-                        out=product[:],
-                        lhsT=x_codes[:, g, s, rows].bitcast(FP8X4),
-                        lhsT_scale=x_scales[:, g, s, rows],
-                        rhs=w_words[:, j, s, g, :].bitcast(FP8X4),
-                        rhs_scale=w_scales[4 * g : P, s, n_cols(j)],
+                        out=v_ps[:],
+                        lhsT=x_codes[:, g, 1, rows].bitcast(FP8X4),
+                        lhsT_scale=x_scales[:, g, 1, rows],
+                        rhs=w_words[:, j, 1, g, :].bitcast(FP8X4),
+                        rhs_scale=w_scales[4 * g : P, 1, n_cols(j)],
                         start=(g == 0),
                         stop=(g == PASSES - 1),
                     )
-                return product
+                return v_ps
 
             def stage_states(i):
                 j, m = divmod(i, ROW_TILES)
-                ab_ps = staged.tile([P, 2, N_BLOCK], BF16)
+                ab_ps = banks.tile([P, 2, N_BLOCK], BF16, tag="ab")
                 for s in range(2):
                     nc.tensor.matmul(
                         out=ab_ps[:, s, :], lhsT=ident[:], rhs=ab_sb[:, j, s, m, :], start=True, stop=True
                     )
                 return ab_ps
 
-            def project(i):
-                return product_of(i, 0), product_of(i, 1), stage_states(i)
-
-
-            def exponents(i, k_ps):
-                j, m = divmod(i, ROW_TILES)
-                first = work.tile([P, 2, N_BLOCK], F32)
-                nc.vector.tensor_tensor(
-                    out=first[:],
-                    in0=uw[:, j, m],
-                    in1=k_ps[:].unsqueeze(1).to_broadcast([P, 2, N_BLOCK]),
-                    op=ALU.subtract,
-                )
-                new_p = work.tile([P, N_BLOCK], F32, bufs=STORE_BUFS_P)
-                nc.vector.tensor_tensor(out=new_p[:], in0=uw[:, j, m, 1, :], in1=k_ps[:], op=ALU.max)
-                nc.sync.dma_start(out=out_4[P * m : P * (m + 1), n_cols(j)], in_=new_p[:])
-                second = work.tile([P, 2, 2, N_BLOCK], F32)
-                nc.scalar.activation(out=second[:, :, 1, :], in_=first[:], func=ACT.Relu)
-                nc.scalar.activation(out=second[:, :, 1, :], in_=second[:, :, 1, :], func=ACT.Exp, scale=-1.0)
-                nc.scalar.activation(out=first[:], in_=first[:], func=ACT.Exp)
-                return first, second
-
             def combine(i, first, second, v_ps, ab_ps):
-                j, m = divmod(i, ROW_TILES)
-                rows = slice(P * m, P * (m + 1))
                 nc.vector.tensor_tensor(
                     out=second[:, :, 0, :],
                     in0=second[:, :, 1, :],
@@ -301,14 +394,25 @@ def tile_rwkv_timemix_for_quant_pa_kernel(
                 nc.sync.dma_start(out=out_b[rows, n_cols(j)], in_=result[:, h, 1, :])
 
             late_sums = []
-            first_k = [product_of(0, 0), product_of(1, 0)]
-            banks_of = {i: (first_k[i], product_of(i, 1), stage_states(i)) for i in range(2)}
-            exps_of = {0: exponents(0, banks_of[0][0])}
+            values = {0: value_of(0)}
+            states = {0: stage_states(0)}
+            exps[1] = exponents(1, splits[0][0], splits[0][1])
+            values[1] = value_of(1)
             for i in range(UNITS):
-                if i + 1 < UNITS:
-                    exps_of[i + 1] = exponents(i + 1, banks_of[i + 1][0])
-                combine(i, exps_of[i][0], exps_of[i][1], banks_of[i][1], banks_of[i][2])
+                j, m = divmod(i, ROW_TILES)
+                if m == 0 and 1 <= j and j + 1 < N_BLOCKS:
+                    splits[j + 1] = split(j + 1, keys)
+                combine(i, exps[i][0], exps[i][1], values[i], states[i])
+                if m == 0 and j + 2 < N_BLOCKS:
+                    turn_states(j + 2)
+                if m == 1 and j + 2 < N_BLOCKS:
+                    keys = keys_of(j + 2)
                 if i + 2 < UNITS:
-                    banks_of[i + 2] = project(i + 2)
+                    jn = (i + 2) // ROW_TILES
+                    exps[i + 2] = exponents(i + 2, splits[jn][0], splits[jn][1])
+                if i + 1 < UNITS:
+                    states[i + 1] = stage_states(i + 1)
+                if i + 2 < UNITS:
+                    values[i + 2] = value_of(i + 2)
             for i, h, result, second in late_sums:
                 add_and_store(nc.vector, i, h, result, second)

@@ -23,7 +23,7 @@ N_BLOCKS = D // N_BLOCK
 UNITS = N_BLOCKS * ROW_TILES
 C_TILES = N_BLOCK // P
 HALVES = 2
-STORE_BUFS_P = 5
+STORE_BUFS_P = 4
 STORE_BUFS_AB = 5
 VECTOR_SUMS = 3
 QUADRANTS = 4
@@ -73,23 +73,28 @@ def tile_rwkv_timemix_for_quant_pa_kernel(
         x_scales = keep.tile([P, PASSES, 2, B], U8, align_bytes=64)
         ab_sb = keep.tile([P, N_BLOCKS, 2, ROW_TILES, N_BLOCK], BF16)
         sp_sb = keep.tile([P, N_BLOCKS, ROW_TILES, N_BLOCK], BF16)
-        sp_turned = keep.tile([P, 2, C_TILES, B], BF16)
-        neg_shift = keep.tile([P, 2, D // P], F32)
+        w_turned = keep.tile([P, 2, C_TILES, B], F32)
+        neg_decay = keep.tile([P, D // P], F32)
+        shift_gap = keep.tile([P, D // P], F32)
         mix_bf = keep.tile([P, 2, PASSES, PACK], BF16)
         mix = keep.tile([P, 2, PASSES * PACK], F32)
         rest = keep.tile([P, 2, PASSES * PACK], F32)
         shift_rows = keep.tile([P, P], BF16)
 
         def turn_states(j):
-            turned_ps = banks.tile([P, C_TILES, B], BF16, tag=("kb", "ka", "ka", "ka")[j])
+            turned_ps = banks.tile([P, C_TILES, B], BF16, tag=("kb", "e2", "e2", "e2")[j])
             for c in range(C_TILES):
                 for m in range(ROW_TILES):
                     nc.tensor.transpose(
                         turned_ps[:, c, P * m : P * (m + 1)], sp_sb[:, j, m, P * c : P * (c + 1)], ident[:]
                     )
-            nc.scalar.copy(out=sp_turned[:, j % 2], in_=turned_ps[:])
+            for c in range(C_TILES):
+                ch = C_TILES * j + c
+                nc.scalar.activation(
+                    out=w_turned[:, j % 2, c, :], in_=turned_ps[:, c, :], func=ACT.Identity, bias=neg_decay[:, ch : ch + 1]
+                )
 
-        with tc.tile_pool(name="inputs", bufs=1) as inputs, tc.tile_pool(name="mixing", bufs=4) as mixing:
+        with tc.tile_pool(name="inputs", bufs=1) as inputs, tc.tile_pool(name="mixing", bufs=3) as mixing:
             x_sb = inputs.tile([P, PASSES, ROW_TILES, K_PASS], BF16)
             sx_sb = inputs.tile([P, PASSES, ROW_TILES, K_PASS], BF16)
             nc.vector.memset(shift_rows[:].bitcast(I32), 0)
@@ -98,8 +103,8 @@ def tile_rwkv_timemix_for_quant_pa_kernel(
             by_row_tile = "(m p) c -> p m c"
             for g in range(PASSES):
                 k_cols = slice(K_PASS * g, K_PASS * (g + 1))
-                nc.sync.dma_start(out=x_sb[:, g], in_=x.rearrange(by_row_tile, p=P)[:, :, k_cols])
                 nc.sync.dma_start(out=sx_sb[:, g], in_=state_x.rearrange(by_row_tile, p=P)[:, :, k_cols])
+                nc.sync.dma_start(out=x_sb[:, g], in_=x.rearrange(by_row_tile, p=P)[:, :, k_cols])
                 if g == 0:
                     for s, time_mix in enumerate((time_mix_k, time_mix_v)):
                         nc.sync.dma_start(
@@ -138,9 +143,11 @@ def tile_rwkv_timemix_for_quant_pa_kernel(
             load_words(1, 0)
             for j in range(N_BLOCKS):
                 load_words(j, 1)
+                if j == 0:
+                    load_p(2)
+                    load_p(3)
                 load_ab(j)
                 if j + 2 < N_BLOCKS:
-                    load_p(j + 2)
                     load_words(j + 2, 0)
 
             nc.vector.tensor_copy(out=mix[:], in_=mix_bf[:].rearrange("p s g t -> p s (g t)"))
@@ -153,37 +160,33 @@ def tile_rwkv_timemix_for_quant_pa_kernel(
                 op1=ALU.add,
             )
 
-            def turn(g):
-                tags = (("p", "s"), ("e0", "e1"), ("v", "ab"), ("p", "s"))
-                views = []
-                for k, source in enumerate((sx_sb, x_sb)):
-                    words = banks.tile([P, HALVES, B], F32, tag=tags[g][k])
-                    for h in range(HALVES):
-                        for m in range(ROW_TILES):
-                            nc.tensor.transpose(
-                                words[:, h, P * m : P * (m + 1)],
-                                source[:, g, m, :].bitcast(F32)[:, h : K_PASS // 2 : HALVES],
-                                ident_words[:],
-                            )
-                    views.append(
-                        words[:].rearrange("p h b -> p (h b)").bitcast(BF16).rearrange("p (h b e) -> p h b e", h=HALVES, e=2)
-                    )
-                return views[1], views[0]
+            def turn(source, g, tag):
+                words = banks.tile([P, HALVES, B], F32, tag=tag)
+                for h in range(HALVES):
+                    for m in range(ROW_TILES):
+                        nc.tensor.transpose(
+                            words[:, h, P * m : P * (m + 1)],
+                            source[:, g, m, :].bitcast(F32)[:, h : K_PASS // 2 : HALVES],
+                            ident_words[:],
+                        )
+                return words
+
+            def by_index(words):
+                return words[:].rearrange("p h b -> p (h b)").bitcast(BF16).rearrange("p (h b e) -> p h b e", h=HALVES, e=2)
 
             def mix_half(g, s, planes):
-                x_turned, sx_turned = turned_tiles[g]
-                sx_share = mixing.tile([P, PACK, B], F32, bufs=4)
+                sx_share = mixing.tile([P, PACK, B], F32)
                 for t in range(PACK):
                     col = PACK * g + t
                     nc.scalar.activation(
                         out=sx_share[:, t, :],
-                        in_=sx_turned[:, t // 2, :, t % 2],
+                        in_=turned_sx[g][:, t // 2, :, t % 2],
                         func=ACT.Copy,
                         scale=rest[:, s, col : col + 1],
                     )
                     nc.vector.scalar_tensor_tensor(
                         out=planes[:, s, t, :],
-                        in0=x_turned[:, t // 2, :, t % 2],
+                        in0=turned_x[g][:, t // 2, :, t % 2],
                         scalar=mix[:, s, col : col + 1],
                         in1=sx_share[:, t, :],
                         op0=ALU.mult,
@@ -213,41 +216,17 @@ def tile_rwkv_timemix_for_quant_pa_kernel(
                     in_=grouped[:, first_s : last_s + 1].rearrange("p s b t -> p (s b t)"),
                 )
 
-            turned_tiles = {0: turn(0)}
+            turned_x, turned_sx = {}, {}
             planes_of, grouped_of = {}, {}
-            shift_ps = banks.tile([P, P], BF16, tag="ka")
-            nc.tensor.transpose(shift_ps[:], shift_rows[:], ident[:])
 
-            def open_round(g):
-                planes = mixing.tile([P, 2, PACK, B], BF16)
-                grouped = mixing.tile([P, 2, B, PACK], BF16, align_bytes=64)
-                planes_of[g], grouped_of[g] = planes, grouped
+            def turn_both(g, tags):
+                turned_sx[g] = by_index(turn(sx_sb, g, tags[0]))
+                turned_x[g] = by_index(turn(x_sb, g, tags[1]))
 
-            turned_tiles[1] = turn(1)
-            turned_tiles[2] = turn(2)
             for g in range(PASSES):
-                open_round(g)
-            mix_half(0, 0, planes_of[0])
-            regroup(planes_of[0], grouped_of[0], 0, 0)
-            mix_half(0, 1, planes_of[0])
-            regroup(planes_of[0], grouped_of[0], 1, 0)
-            spread = shift_ps[:, 0:32].rearrange("p (h c) -> p h c", h=2)
-            decay = keep.tile([P, D // P], F32)
-            nc.scalar.activation(out=decay[:], in_=spread[:, 1], func=ACT.Exp)
-            nc.vector.tensor_scalar_mul(neg_shift[:, 0], spread[:, 0], -1.0)
-            nc.vector.tensor_scalar_mul(neg_shift[:, 1], decay[:], -1.0)
-            turned_tiles[3] = turn(3)
-            mix_half(1, 0, planes_of[1])
-            regroup(planes_of[1], grouped_of[1], 0, 0)
-            quantise(0, grouped_of[0], 0, 1)
-            mix_half(2, 0, planes_of[2])
-            regroup(planes_of[2], grouped_of[2], 0, 0)
-            quantise(1, grouped_of[1], 0, 0)
-            mix_half(3, 0, planes_of[3])
-            turn_states(0)
-            regroup(planes_of[3], grouped_of[3], 0, 1)
-            quantise(2, grouped_of[2], 0, 0)
-            quantise(3, grouped_of[3], 0, 0)
+                planes = mixing.tile([P, 2, PACK, B], BF16, bufs=4)
+                grouped = mixing.tile([P, 2, B, PACK], BF16, bufs=4, align_bytes=64)
+                planes_of[g], grouped_of[g] = planes, grouped
 
             def keys_of(j):
                 pair = []
@@ -268,80 +247,125 @@ def tile_rwkv_timemix_for_quant_pa_kernel(
                     pair.append(k_ps)
                 return pair
 
-            def split(j, keys):
-                z = keep.tile([P, C_TILES, B], F32, bufs=2)
-                new_p = keep.tile([P, C_TILES, B], F32, bufs=2)
+            g_of, p_of = {}, {}
+
+            def new_states(j, keys, op):
+                out = keep.tile([P, C_TILES, B], F32, tag=("g_turned" if op == ALU.subtract else "p_turned"), bufs=2)
                 for half in range(2):
-                    nc.vector.tensor_tensor(
-                        out=z[:, 2 * half : 2 * half + 2],
-                        in0=sp_turned[:, j % 2, 2 * half : 2 * half + 2],
-                        in1=keys[half][:],
-                        op=ALU.subtract,
+                    two = slice(2 * half, 2 * half + 2)
+                    nc.vector.tensor_tensor(out=out[:, two], in0=w_turned[:, j % 2, two], in1=keys[half][:], op=op)
+                (g_of if op == ALU.subtract else p_of)[j] = out
+
+            def split(j, keys):
+                new_states(j, keys, ALU.subtract)
+                new_states(j, keys, ALU.max)
+
+            def stage_states(i):
+                j, m = divmod(i, ROW_TILES)
+                ab_ps = banks.tile([P, 2, N_BLOCK], BF16, tag="ab")
+                for s in range(2):
+                    nc.tensor.matmul(
+                        out=ab_ps[:, s, :], lhsT=ident[:], rhs=ab_sb[:, j, s, m, :], start=True, stop=True
                     )
+                return ab_ps
+
+
+            def turned_sum(tag, left, right):
+                total = banks.tile([P, N_BLOCK], F32, tag=tag)
                 for c in range(C_TILES):
-                    ch = C_TILES * j + c
-                    nc.vector.scalar_tensor_tensor(
-                        out=new_p[:, c, :],
-                        in0=sp_turned[:, j % 2, c, :],
-                        scalar=neg_shift[:, 1, ch : ch + 1],
-                        in1=keys[c // 2][:, c % 2, :],
-                        op0=ALU.add,
-                        op1=ALU.max,
+                    cols = slice(P * c, P * (c + 1))
+                    nc.tensor.matmul(
+                        out=total[:, cols], lhsT=left(c), rhs=ident_words[:],
+                        start=True, stop=(right is None), is_transpose=True,
                     )
-                return z, new_p
+                    if right is not None:
+                        nc.tensor.matmul(
+                            out=total[:, cols], lhsT=right(c), rhs=ident_words[:],
+                            start=False, stop=True, is_transpose=True,
+                        )
+                return total
 
-
-            def exponents(i, z, new_p):
+            def exponents(i):
                 j, m = divmod(i, ROW_TILES)
                 rows = slice(P * m, P * (m + 1))
                 first = keep.tile([P, 2, N_BLOCK], F32, bufs=3)
                 second = keep.tile([P, 2, 2, N_BLOCK], F32, bufs=3)
-                for h in range(2):
-                    e_ps = banks.tile([P, N_BLOCK], F32, tag=("e0", "e1")[h])
-                    for c in range(C_TILES):
-                        cols = slice(P * c, P * (c + 1))
-                        ch = C_TILES * j + c
-                        nc.tensor.matmul(
-                            out=e_ps[:, cols], lhsT=z[:, c, rows], rhs=ident_words[:],
-                            start=True, stop=False, is_transpose=True,
-                        )
-                        nc.tensor.matmul(
-                            out=e_ps[:, cols], lhsT=neg_shift[:, h, ch : ch + 1].to_broadcast([P, P]), rhs=ident_words[:],
-                            start=False, stop=True, is_transpose=True,
-                        )
-                    nc.scalar.activation(out=second[:, h, 1, :], in_=e_ps[:], func=ACT.Relu)
+
+                def gap(c):
+                    ch = C_TILES * j + c
+                    return shift_gap[:, ch : ch + 1].to_broadcast([P, P])
+
+                for h, right in ((1, None), (0, gap)):
+                    e_ps = turned_sum(("e0", "e1")[h], lambda c: g_of[j][:, c, rows], right)
                     nc.scalar.activation(out=first[:, h, :], in_=e_ps[:], func=ACT.Exp)
-                    nc.scalar.activation(out=second[:, h, 1, :], in_=second[:, h, 1, :], func=ACT.Exp, scale=-1.0)
-                p_ps = banks.tile([P, N_BLOCK], F32, tag="p")
-                for c in range(C_TILES):
-                    nc.tensor.transpose(p_ps[:, P * c : P * (c + 1)], new_p[:, c, rows], ident_words[:])
+                    nc.scalar.activation(out=second[:, 1, h, :], in_=e_ps[:], func=ACT.Relu)
+                nc.scalar.activation(out=second[:, 1], in_=second[:, 1], func=ACT.Exp, scale=-1.0)
+                return first, second
+
+            def emit_p(i):
+                j, m = divmod(i, ROW_TILES)
+                rows = slice(P * m, P * (m + 1))
+                p_ps = turned_sum("p", lambda c: p_of[j][:, c, rows], None)
                 p_out = keep.tile([P, N_BLOCK], F32, bufs=STORE_BUFS_P)
                 nc.scalar.copy(out=p_out[:], in_=p_ps[:])
                 nc.sync.dma_start(out=out_4[rows, n_cols(j)], in_=p_out[:])
-                return first, second
 
+            def turn_shifts():
+                shift_ps = banks.tile([P, P], BF16, tag="ka")
+                nc.tensor.transpose(shift_ps[:], shift_rows[:], ident[:])
+                spread = shift_ps[:, 0:32].rearrange("p (h c) -> p h c", h=2)
+                decay = keep.tile([P, D // P], F32)
+                nc.scalar.activation(out=decay[:], in_=spread[:, 1], func=ACT.Exp)
+                nc.vector.tensor_scalar_mul(neg_decay[:], decay[:], -1.0)
+                nc.vector.tensor_tensor(out=shift_gap[:], in0=spread[:, 0], in1=neg_decay[:], op=ALU.add)
+                nc.vector.tensor_scalar_mul(shift_gap[:], shift_gap[:], -1.0)
+
+            exps, states, values, results = {}, {}, {}, {}
+            turn_both(0, ("p", "e2"))
+            turn_both(1, ("e0", "e1"))
+            mix_half(0, 1, planes_of[0])
+            mix_half(0, 0, planes_of[0])
+            turn_shifts()
+            mix_half(1, 0, planes_of[1])
+            turn_both(2, ("v", "ab"))
+            regroup(planes_of[0], grouped_of[0], 1, 0)
+            mix_half(2, 0, planes_of[2])
+            turn_both(3, ("p", "e2"))
+            mix_half(3, 0, planes_of[3])
+            regroup(planes_of[0], grouped_of[0], 0, 0)
+            regroup(planes_of[1], grouped_of[1], 0, 0)
+            quantise(1, grouped_of[1], 0, 0)
+            quantise(0, grouped_of[0], 0, 0)
+            turn_states(0)
+            regroup(planes_of[3], grouped_of[3], 0, 1)
+            regroup(planes_of[2], grouped_of[2], 0, 0)
+            quantise(2, grouped_of[2], 0, 0)
+            quantise(3, grouped_of[3], 0, 0)
+            quantise(0, grouped_of[0], 1, 1)
             mix_half(1, 1, planes_of[1])
-            regroup(planes_of[1], grouped_of[1], 1, 0)
-            turn_states(1)
             keys = keys_of(0)
+            new_states(0, keys, ALU.subtract)
             mix_half(3, 1, planes_of[3])
+            regroup(planes_of[1], grouped_of[1], 1, 0)
             regroup(planes_of[3], grouped_of[3], 1, 0)
-            splits = {0: split(0, keys)}
             mix_half(2, 1, planes_of[2])
-            exps = {0: exponents(0, splits[0][0], splits[0][1])}
-            keys = keys_of(1)
-            quantise(1, grouped_of[1], 1, 1)
-            regroup(planes_of[2], grouped_of[2], 1, 1)
+            new_states(0, keys, ALU.max)
             quantise(3, grouped_of[3], 1, 1)
+            quantise(1, grouped_of[1], 1, 1)
+            exps[0] = exponents(0)
+            turn_states(1)
+            regroup(planes_of[2], grouped_of[2], 1, 0)
             quantise(2, grouped_of[2], 1, 1)
-            splits[1] = split(1, keys)
+            exps[1] = exponents(1)
+            states[0] = stage_states(0)
+            keys = keys_of(1)
 
         with tc.tile_pool(name="work", bufs=3, reuse_waits="tile") as work:
 
             def value_of(i):
                 j, m = divmod(i, ROW_TILES)
                 rows = slice(P * m, P * (m + 1))
-                v_ps = banks.tile([P, N_BLOCK], F32, tag=("v", "s")[i % 2])
+                v_ps = banks.tile([P, N_BLOCK], F32, tag="v")
                 for g in range(PASSES):
                     nc.tensor.matmul_mx(
                         out=v_ps[:],
@@ -354,65 +378,69 @@ def tile_rwkv_timemix_for_quant_pa_kernel(
                     )
                 return v_ps
 
-            def stage_states(i):
-                j, m = divmod(i, ROW_TILES)
-                ab_ps = banks.tile([P, 2, N_BLOCK], BF16, tag="ab")
-                for s in range(2):
-                    nc.tensor.matmul(
-                        out=ab_ps[:, s, :], lhsT=ident[:], rhs=ab_sb[:, j, s, m, :], start=True, stop=True
-                    )
-                return ab_ps
-
-            def combine(i, first, second, v_ps, ab_ps):
-                nc.vector.tensor_tensor(
-                    out=second[:, :, 0, :],
-                    in0=second[:, :, 1, :],
-                    in1=v_ps[:].unsqueeze(1).to_broadcast([P, 2, N_BLOCK]),
-                    op=ALU.mult,
-                )
+            def state_terms(i, first, second, ab_ps):
                 result = work.tile([P, 2, 2, N_BLOCK], F32, bufs=STORE_BUFS_AB)
                 for h in range(2):
                     nc.vector.scalar_tensor_tensor(
-                        out=result[:, h],
+                        out=result[:, :, h, :],
                         in0=first[:, h, :].unsqueeze(1).to_broadcast([P, 2, N_BLOCK]),
                         scalar=1.0,
                         in1=ab_ps[:],
                         op0=ALU.min,
                         op1=ALU.mult,
                     )
-                    if 2 * i + h < 2 * UNITS - VECTOR_SUMS:
-                        add_and_store(nc.gpsimd, i, h, result, second)
-                    else:
-                        late_sums.append((i, h, result, second))
+                add_and_store(i, 1, result, second)
+                return result
 
-            def add_and_store(adder, i, h, result, second):
+            def value_terms(i, result, second, v_ps):
+                nc.vector.tensor_tensor(
+                    out=second[:, 0],
+                    in0=second[:, 1],
+                    in1=v_ps[:].unsqueeze(1).to_broadcast([P, 2, N_BLOCK]),
+                    op=ALU.mult,
+                )
+                add_and_store(i, 0, result, second)
+
+            def add_and_store(i, s, result, second):
+                count = 2 * i + 1 - s
+                if count >= 2 * UNITS - VECTOR_SUMS and not late:
+                    late_sums.append((i, s, result, second))
+                    return
                 j, m = divmod(i, ROW_TILES)
                 rows = slice(P * m, P * (m + 1))
-                out_a, out_b = ((out_0, out_1), (out_2, out_3))[h]
-                adder.tensor_tensor(out=result[:, h], in0=result[:, h], in1=second[:, h], op=ALU.add)
-                nc.sync.dma_start(out=out_a[rows, n_cols(j)], in_=result[:, h, 0, :])
-                nc.sync.dma_start(out=out_b[rows, n_cols(j)], in_=result[:, h, 1, :])
+                adder = nc.vector if late else nc.gpsimd
+                adder.tensor_tensor(out=result[:, s], in0=result[:, s], in1=second[:, s], op=ALU.add)
+                for h, out in enumerate(((out_0, out_2), (out_1, out_3))[s]):
+                    nc.sync.dma_start(out=out[rows, n_cols(j)], in_=result[:, s, h, :])
 
+            late = []
             late_sums = []
-            values = {0: value_of(0)}
-            states = {0: stage_states(0)}
-            exps[1] = exponents(1, splits[0][0], splits[0][1])
-            values[1] = value_of(1)
-            for i in range(UNITS):
-                j, m = divmod(i, ROW_TILES)
-                if m == 0 and 1 <= j and j + 1 < N_BLOCKS:
-                    splits[j + 1] = split(j + 1, keys)
-                combine(i, exps[i][0], exps[i][1], values[i], states[i])
-                if m == 0 and j + 2 < N_BLOCKS:
+            for j in range(N_BLOCKS):
+                first_unit, second_unit = ROW_TILES * j, ROW_TILES * j + 1
+                more = j + 1 < N_BLOCKS
+                values[first_unit] = value_of(first_unit)
+                if j + 2 < N_BLOCKS:
                     turn_states(j + 2)
-                if m == 1 and j + 2 < N_BLOCKS:
-                    keys = keys_of(j + 2)
-                if i + 2 < UNITS:
-                    jn = (i + 2) // ROW_TILES
-                    exps[i + 2] = exponents(i + 2, splits[jn][0], splits[jn][1])
-                if i + 1 < UNITS:
-                    states[i + 1] = stage_states(i + 1)
-                if i + 2 < UNITS:
-                    values[i + 2] = value_of(i + 2)
-            for i, h, result, second in late_sums:
-                add_and_store(nc.vector, i, h, result, second)
+                emit_p(first_unit)
+                results[first_unit] = state_terms(first_unit, exps[first_unit][0], exps[first_unit][1], states[first_unit])
+                if more:
+                    new_states(j + 1, keys, ALU.subtract)
+                states[second_unit] = stage_states(second_unit)
+                if more:
+                    exps[first_unit + 2] = exponents(first_unit + 2)
+                value_terms(first_unit, results[first_unit], exps[first_unit][1], values[first_unit])
+                values[second_unit] = value_of(second_unit)
+                emit_p(second_unit)
+                results[second_unit] = state_terms(
+                    second_unit, exps[second_unit][0], exps[second_unit][1], states[second_unit]
+                )
+                if more:
+                    new_states(j + 1, keys, ALU.max)
+                    states[first_unit + 2] = stage_states(first_unit + 2)
+                    if j + 2 < N_BLOCKS:
+                        keys = keys_of(j + 2)
+                    exps[second_unit + 2] = exponents(second_unit + 2)
+                value_terms(second_unit, results[second_unit], exps[second_unit][1], values[second_unit])
+            late.append(True)
+            for i, s, result, second in late_sums:
+                add_and_store(i, s, result, second)

@@ -67,18 +67,18 @@ def tile_rwkv_timemix_for_quant_pa_kernel(
         nc.vector.memset(warm[:], 0.0)
         nc.scalar.activation(out=warm[:], in_=warm[:], func=ACT.Exp)
 
-        w_words = keep.tile([P, N_BLOCKS, 2, PASSES, N_BLOCK], U32, align_bytes=64)
+        w_words = {}
         w_scales = keep.tile([P, 2, D], U8, align_bytes=64)
         x_codes = keep.tile([P, PASSES, 2, B], U32, align_bytes=64)
         x_scales = keep.tile([P, PASSES, 2, B], U8, align_bytes=64)
-        ab_sb = keep.tile([P, N_BLOCKS, 2, ROW_TILES, N_BLOCK], BF16)
-        sp_sb = keep.tile([P, N_BLOCKS, ROW_TILES, N_BLOCK], BF16)
+        ab_sb = keep.tile([P, 2, 2, ROW_TILES, 2 * N_BLOCK], BF16)
+        sp_sb = keep.tile([P, 2, ROW_TILES, 2 * N_BLOCK], BF16)
         w_turned = keep.tile([P, 2, C_TILES, B], F32)
         neg_decay = keep.tile([P, D // P], F32)
         shift_gap = keep.tile([P, D // P], F32)
-        mix_bf = keep.tile([P, 2, PASSES, PACK], BF16)
-        mix = keep.tile([P, 2, PASSES * PACK], F32)
-        rest = keep.tile([P, 2, PASSES * PACK], F32)
+        mix_rows = keep.tile([P, K_PASS], BF16)
+        mix = keep.tile([P, PACK, 2 * PASSES], F32)
+        rest = keep.tile([P, PACK, 2 * PASSES], F32)
         shift_rows = keep.tile([P, P], BF16)
 
         def turn_states(j):
@@ -86,7 +86,7 @@ def tile_rwkv_timemix_for_quant_pa_kernel(
             for c in range(C_TILES):
                 for m in range(ROW_TILES):
                     nc.tensor.transpose(
-                        turned_ps[:, c, P * m : P * (m + 1)], sp_sb[:, j, m, P * c : P * (c + 1)], ident[:]
+                        turned_ps[:, c, P * m : P * (m + 1)], sp_sb[:, j // 2, m, N_BLOCK * (j % 2) + P * c : N_BLOCK * (j % 2) + P * (c + 1)], ident[:]
                     )
             for c in range(C_TILES):
                 ch = C_TILES * j + c
@@ -95,27 +95,25 @@ def tile_rwkv_timemix_for_quant_pa_kernel(
                 )
 
         with tc.tile_pool(name="inputs", bufs=1) as inputs, tc.tile_pool(name="mixing", bufs=3) as mixing:
-            x_sb = inputs.tile([P, PASSES, ROW_TILES, K_PASS], BF16)
-            sx_sb = inputs.tile([P, PASSES, ROW_TILES, K_PASS], BF16)
+            pieces = ((0, 1), (1, 1), (2, 2))
+            x_sb, sx_sb = {}, {}
+            for first_pass, count in pieces:
+                x_piece = inputs.tile([P, ROW_TILES, K_PASS * count], BF16, tag="x" + str(first_pass))
+                sx_piece = inputs.tile([P, ROW_TILES, K_PASS * count], BF16, tag="sx" + str(first_pass))
+                for g in range(first_pass, first_pass + count):
+                    start = K_PASS * (g - first_pass)
+                    x_sb[g], sx_sb[g] = (x_piece, start), (sx_piece, start)
+            nc.vector.memset(mix_rows[:].bitcast(I32), 0)
             nc.vector.memset(shift_rows[:].bitcast(I32), 0)
             nc.vector.memset(w_scales[:].bitcast(I32), 0)
 
             by_row_tile = "(m p) c -> p m c"
-            for g in range(PASSES):
-                k_cols = slice(K_PASS * g, K_PASS * (g + 1))
-                nc.sync.dma_start(out=sx_sb[:, g], in_=state_x.rearrange(by_row_tile, p=P)[:, :, k_cols])
-                nc.sync.dma_start(out=x_sb[:, g], in_=x.rearrange(by_row_tile, p=P)[:, :, k_cols])
-                if g == 0:
-                    for s, time_mix in enumerate((time_mix_k, time_mix_v)):
-                        nc.sync.dma_start(
-                            out=mix_bf[:, s], in_=time_mix[0].rearrange("(g p t) -> p g t", g=PASSES, p=P)
-                        )
-                    for s, vector in enumerate((time_first, time_decay)):
-                        nc.sync.dma_start(
-                            out=shift_rows[16 * s : 16 * (s + 1), :], in_=vector.rearrange("(c p) -> c p", p=P)
-                        )
-            def load_p(j):
-                nc.sync.dma_start(out=sp_sb[:, j], in_=state_p.rearrange(by_row_tile, p=P)[:, :, n_cols(j)])
+
+            def pair_cols(q):
+                return slice(2 * N_BLOCK * q, 2 * N_BLOCK * (q + 1))
+
+            def load_p(q):
+                nc.sync.dma_start(out=sp_sb[:, q], in_=state_p.rearrange(by_row_tile, p=P)[:, :, pair_cols(q)])
 
             def load_scales(s):
                 for quad in range(QUADRANTS):
@@ -124,49 +122,60 @@ def tile_rwkv_timemix_for_quant_pa_kernel(
                         in_=weights[s][1][:, 4 * quad : 4 * quad + 4, :].bitcast(I32),
                     )
 
-            def load_words(j, s):
+            def load_words(first_block, count, s):
+                piece = keep.tile([P, PASSES, N_BLOCK * count], U32, tag="w%d%d" % (s, first_block), align_bytes=64)
                 words = weights[s][0].rearrange("g p n t -> p g (n t)")
-                nc.sync.dma_start(
-                    out=w_words[:, j, s].bitcast(I32),
-                    in_=words[:, :, PACK * N_BLOCK * j : PACK * N_BLOCK * (j + 1)].bitcast(I32),
-                )
+                cols = slice(PACK * N_BLOCK * first_block, PACK * N_BLOCK * (first_block + count))
+                nc.sync.dma_start(out=piece[:].bitcast(I32), in_=words[:, :, cols].bitcast(I32))
+                for j in range(first_block, first_block + count):
+                    w_words[s, j] = (piece, N_BLOCK * (j - first_block))
 
-            def load_ab(j):
+            def load_ab(q):
                 for s, state in enumerate((state_A, state_B)):
-                    nc.sync.dma_start(out=ab_sb[:, j, s], in_=state.rearrange(by_row_tile, p=P)[:, :, n_cols(j)])
+                    nc.sync.dma_start(out=ab_sb[:, q, s], in_=state.rearrange(by_row_tile, p=P)[:, :, pair_cols(q)])
 
+            for s, time_mix in enumerate((time_mix_k, time_mix_v)):
+                nc.sync.dma_start(
+                    out=mix_rows[PASSES * s : PASSES * (s + 1), :], in_=time_mix[0].rearrange("(g k) -> g k", g=PASSES)
+                )
+            for first_pass, count in pieces:
+                k_cols = slice(K_PASS * first_pass, K_PASS * (first_pass + count))
+                nc.sync.dma_start(out=sx_sb[first_pass][0][:], in_=state_x.rearrange(by_row_tile, p=P)[:, :, k_cols])
+                nc.sync.dma_start(out=x_sb[first_pass][0][:], in_=x.rearrange(by_row_tile, p=P)[:, :, k_cols])
+                if first_pass == 1:
+                    for s, vector in enumerate((time_first, time_decay)):
+                        nc.sync.dma_start(
+                            out=shift_rows[16 * s : 16 * (s + 1), :], in_=vector.rearrange("(c p) -> c p", p=P)
+                        )
             load_p(0)
-            load_p(1)
             load_scales(0)
-            load_words(0, 0)
+            load_words(0, 1, 0)
+            load_ab(0)
+            load_words(1, 1, 0)
             load_scales(1)
-            load_words(1, 0)
-            for j in range(N_BLOCKS):
-                load_words(j, 1)
-                if j == 0:
-                    load_p(2)
-                    load_p(3)
-                load_ab(j)
-                if j + 2 < N_BLOCKS:
-                    load_words(j + 2, 0)
+            load_words(0, 1, 1)
+            load_p(1)
+            load_words(2, 2, 0)
+            load_words(1, 1, 1)
+            load_ab(1)
+            load_words(2, 2, 1)
 
-            nc.vector.tensor_copy(out=mix[:], in_=mix_bf[:].rearrange("p s g t -> p s (g t)"))
+            mix_ps = banks.tile([P, PACK, P], BF16, tag="kb")
+            for t in range(PACK):
+                nc.tensor.transpose(mix_ps[:, t, :], mix_rows[:, t:K_PASS:PACK], ident[:])
             nc.vector.tensor_scalar(
-                out=rest[:],
-                in0=mix_bf[:].rearrange("p s g t -> p s (g t)"),
-                scalar1=-1.0,
-                scalar2=1.0,
-                op0=ALU.mult,
-                op1=ALU.add,
+                out=rest[:], in0=mix_ps[:, :, 0 : 2 * PASSES], scalar1=-1.0, scalar2=1.0, op0=ALU.mult, op1=ALU.add
             )
+            nc.vector.tensor_copy(out=mix[:], in_=mix_ps[:, :, 0 : 2 * PASSES])
 
             def turn(source, g, tag):
+                piece, start = source[g]
                 words = banks.tile([P, HALVES, B], F32, tag=tag)
                 for h in range(HALVES):
                     for m in range(ROW_TILES):
                         nc.tensor.transpose(
                             words[:, h, P * m : P * (m + 1)],
-                            source[:, g, m, :].bitcast(F32)[:, h : K_PASS // 2 : HALVES],
+                            piece[:, m, start : start + K_PASS].bitcast(F32)[:, h : K_PASS // 2 : HALVES],
                             ident_words[:],
                         )
                 return words
@@ -177,17 +186,17 @@ def tile_rwkv_timemix_for_quant_pa_kernel(
             def mix_half(g, s, planes):
                 sx_share = mixing.tile([P, PACK, B], F32)
                 for t in range(PACK):
-                    col = PACK * g + t
+                    col = PASSES * s + g
                     nc.scalar.activation(
                         out=sx_share[:, t, :],
                         in_=turned_sx[g][:, t // 2, :, t % 2],
                         func=ACT.Copy,
-                        scale=rest[:, s, col : col + 1],
+                        scale=rest[:, t, col : col + 1],
                     )
                     nc.vector.scalar_tensor_tensor(
                         out=planes[:, s, t, :],
                         in0=turned_x[g][:, t // 2, :, t % 2],
-                        scalar=mix[:, s, col : col + 1],
+                        scalar=mix[:, t, col : col + 1],
                         in1=sx_share[:, t, :],
                         op0=ALU.mult,
                         op1=ALU.add,
@@ -237,7 +246,7 @@ def tile_rwkv_timemix_for_quant_pa_kernel(
                         for g in range(PASSES):
                             nc.tensor.matmul_mx(
                                 out=k_ps[:, e, :],
-                                lhsT=w_words[:, j, 0, g, P * c : P * (c + 1)].bitcast(FP8X4),
+                                lhsT=w_words[0, j][0][:, g, w_words[0, j][1] + P * c : w_words[0, j][1] + P * (c + 1)].bitcast(FP8X4),
                                 lhsT_scale=w_scales[4 * g : P, 0, N_BLOCK * j + P * c : N_BLOCK * j + P * (c + 1)],
                                 rhs=x_codes[:, g, 0, :].bitcast(FP8X4),
                                 rhs_scale=x_scales[:, g, 0, :],
@@ -265,7 +274,7 @@ def tile_rwkv_timemix_for_quant_pa_kernel(
                 ab_ps = banks.tile([P, 2, N_BLOCK], BF16, tag="ab")
                 for s in range(2):
                     nc.tensor.matmul(
-                        out=ab_ps[:, s, :], lhsT=ident[:], rhs=ab_sb[:, j, s, m, :], start=True, stop=True
+                        out=ab_ps[:, s, :], lhsT=ident[:], rhs=ab_sb[:, j // 2, s, m, N_BLOCK * (j % 2) : N_BLOCK * (j % 2 + 1)], start=True, stop=True
                     )
                 return ab_ps
 
@@ -371,7 +380,7 @@ def tile_rwkv_timemix_for_quant_pa_kernel(
                         out=v_ps[:],
                         lhsT=x_codes[:, g, 1, rows].bitcast(FP8X4),
                         lhsT_scale=x_scales[:, g, 1, rows],
-                        rhs=w_words[:, j, 1, g, :].bitcast(FP8X4),
+                        rhs=w_words[1, j][0][:, g, w_words[1, j][1] : w_words[1, j][1] + N_BLOCK].bitcast(FP8X4),
                         rhs_scale=w_scales[4 * g : P, 1, n_cols(j)],
                         start=(g == 0),
                         stop=(g == PASSES - 1),

@@ -23,8 +23,8 @@ N_BLOCKS = D // N_BLOCK
 UNITS = N_BLOCKS * ROW_TILES
 C_TILES = N_BLOCK // P
 HALVES = 2
-STORE_BUFS_P = 4
-STORE_BUFS_AB = 5
+STORE_BUFS_P = 8
+STORE_BUFS_AB = 7
 VECTOR_SUMS = 3
 QUADRANTS = 4
 
@@ -315,7 +315,7 @@ def tile_rwkv_timemix_for_quant_pa_kernel(
                 j, m = divmod(i, ROW_TILES)
                 rows = slice(P * m, P * (m + 1))
                 p_ps = turned_sum("p", lambda c: p_of[j][:, c, rows], None)
-                p_out = keep.tile([P, N_BLOCK], F32, bufs=STORE_BUFS_P)
+                p_out = work.tile([P, N_BLOCK], F32, bufs=STORE_BUFS_P)
                 nc.scalar.copy(out=p_out[:], in_=p_ps[:])
                 nc.sync.dma_start(out=out_4[rows, n_cols(j)], in_=p_out[:])
 

import concourse.mybir as mybir
from concourse.masks import make_identity

F32 = mybir.dt.float32
BF16 = mybir.dt.bfloat16
I32 = mybir.dt.int32
U32 = mybir.dt.uint32
U8 = mybir.dt.uint8
FP8X4 = mybir.dt.float8_e4m3fn_x4
ALU = mybir.AluOpType
ACT = mybir.ActivationFunctionType

P = 128
B = 256
E = 2048
D = 2048
PACK = 4
K_PASS = P * PACK
PASSES = E // K_PASS
ROW_TILES = B // P
N_BLOCK = 512
N_BLOCKS = D // N_BLOCK
UNITS = N_BLOCKS * ROW_TILES
C_TILES = N_BLOCK // P
HALVES = 2
STORE_BUFS_P = 8
STORE_BUFS_AB = 7
VECTOR_SUMS = 3
QUADRANTS = 4

FLOPS = 2 * 2 * B * E * D


def tile_rwkv_timemix_for_quant_pa_kernel(
    tc,
    x,
    state_A,
    state_B,
    state_p,
    state_x,
    time_decay,
    time_first,
    time_mix_k,
    time_mix_v,
    W_key_words,
    W_key_scales,
    W_value_words,
    W_value_scales,
    out_0,
    out_1,
    out_2,
    out_3,
    out_4,
):
    nc = tc.nc
    weights = ((W_key_words, W_key_scales), (W_value_words, W_value_scales))

    def n_cols(j):
        return slice(N_BLOCK * j, N_BLOCK * (j + 1))

    with tc.manual_schedule(), tc.tile_pool(name="keep", bufs=1) as keep, tc.psum_pool(name="banks", bufs=1) as banks:
        ident = keep.tile([P, P], BF16)
        make_identity(nc, ident[:])
        ident_words = keep.tile([P, P], F32)
        make_identity(nc, ident_words[:])
        warm = keep.tile([P, 1], F32)
        nc.vector.memset(warm[:], 0.0)
        nc.scalar.activation(out=warm[:], in_=warm[:], func=ACT.Exp)

        w_words = {}
        w_scales = keep.tile([P, 2, D], U8, align_bytes=64)
        x_codes = keep.tile([P, PASSES, 2, B], U32, align_bytes=64)
        x_scales = keep.tile([P, PASSES, 2, B], U8, align_bytes=64)
        ab_sb = keep.tile([P, 2, 2, ROW_TILES, 2 * N_BLOCK], BF16)
        sp_sb = keep.tile([P, 2, ROW_TILES, 2 * N_BLOCK], BF16)
        w_turned = keep.tile([P, 2, C_TILES, B], F32)
        neg_decay = keep.tile([P, D // P], F32)
        shift_gap = keep.tile([P, D // P], F32)
        mix_rows = keep.tile([P, K_PASS], BF16)
        mix = keep.tile([P, PACK, 2 * PASSES], F32)
        rest = keep.tile([P, PACK, 2 * PASSES], F32)
        shift_rows = keep.tile([P, P], BF16)

        def turn_states(j):
            turned_ps = banks.tile([P, C_TILES, B], BF16, tag=("kb", "e2", "e2", "e2")[j])
            for c in range(C_TILES):
                for m in range(ROW_TILES):
                    nc.tensor.transpose(
                        turned_ps[:, c, P * m : P * (m + 1)], sp_sb[:, j // 2, m, N_BLOCK * (j % 2) + P * c : N_BLOCK * (j % 2) + P * (c + 1)], ident[:]
                    )
            for c in range(C_TILES):
                ch = C_TILES * j + c
                nc.scalar.activation(
                    out=w_turned[:, j % 2, c, :], in_=turned_ps[:, c, :], func=ACT.Identity, bias=neg_decay[:, ch : ch + 1]
                )

        with tc.tile_pool(name="inputs", bufs=1) as inputs, tc.tile_pool(name="mixing", bufs=3) as mixing:
            pieces = ((0, 1), (1, 1), (2, 2))
            x_sb, sx_sb = {}, {}
            for first_pass, count in pieces:
                x_piece = inputs.tile([P, ROW_TILES, K_PASS * count], BF16, tag="x" + str(first_pass))
                sx_piece = inputs.tile([P, ROW_TILES, K_PASS * count], BF16, tag="sx" + str(first_pass))
                for g in range(first_pass, first_pass + count):
                    start = K_PASS * (g - first_pass)
                    x_sb[g], sx_sb[g] = (x_piece, start), (sx_piece, start)
            nc.vector.memset(mix_rows[:].bitcast(I32), 0)
            nc.vector.memset(shift_rows[:].bitcast(I32), 0)
            nc.vector.memset(w_scales[:].bitcast(I32), 0)

            by_row_tile = "(m p) c -> p m c"

            def pair_cols(q):
                return slice(2 * N_BLOCK * q, 2 * N_BLOCK * (q + 1))

            def load_p(q):
                nc.sync.dma_start(out=sp_sb[:, q], in_=state_p.rearrange(by_row_tile, p=P)[:, :, pair_cols(q)])

            def load_scales(s):
                for quad in range(QUADRANTS):
                    nc.sync.dma_start(
                        out=w_scales[32 * quad : 32 * quad + 16, s, :].bitcast(I32),
                        in_=weights[s][1][:, 4 * quad : 4 * quad + 4, :].bitcast(I32),
                    )

            def load_words(first_block, count, s):
                piece = keep.tile([P, PASSES, N_BLOCK * count], U32, tag="w%d%d" % (s, first_block), align_bytes=64)
                words = weights[s][0].rearrange("g p n t -> p g (n t)")
                cols = slice(PACK * N_BLOCK * first_block, PACK * N_BLOCK * (first_block + count))
                nc.sync.dma_start(out=piece[:].bitcast(I32), in_=words[:, :, cols].bitcast(I32))
                for j in range(first_block, first_block + count):
                    w_words[s, j] = (piece, N_BLOCK * (j - first_block))

            def load_ab(q):
                for s, state in enumerate((state_A, state_B)):
                    nc.sync.dma_start(out=ab_sb[:, q, s], in_=state.rearrange(by_row_tile, p=P)[:, :, pair_cols(q)])

            for s, time_mix in enumerate((time_mix_k, time_mix_v)):
                nc.sync.dma_start(
                    out=mix_rows[PASSES * s : PASSES * (s + 1), :], in_=time_mix[0].rearrange("(g k) -> g k", g=PASSES)
                )
            for first_pass, count in pieces:
                k_cols = slice(K_PASS * first_pass, K_PASS * (first_pass + count))
                nc.sync.dma_start(out=sx_sb[first_pass][0][:], in_=state_x.rearrange(by_row_tile, p=P)[:, :, k_cols])
                nc.sync.dma_start(out=x_sb[first_pass][0][:], in_=x.rearrange(by_row_tile, p=P)[:, :, k_cols])
                if first_pass == 1:
                    for s, vector in enumerate((time_first, time_decay)):
                        nc.sync.dma_start(
                            out=shift_rows[16 * s : 16 * (s + 1), :], in_=vector.rearrange("(c p) -> c p", p=P)
                        )
            load_p(0)
            load_scales(0)
            load_words(0, 1, 0)
            load_ab(0)
            load_words(1, 1, 0)
            load_scales(1)
            load_words(0, 1, 1)
            load_p(1)
            load_words(2, 2, 0)
            load_words(1, 1, 1)
            load_ab(1)
            load_words(2, 2, 1)

            mix_ps = banks.tile([P, PACK, P], BF16, tag="kb")
            for t in range(PACK):
                nc.tensor.transpose(mix_ps[:, t, :], mix_rows[:, t:K_PASS:PACK], ident[:])
            nc.vector.tensor_scalar(
                out=rest[:], in0=mix_ps[:, :, 0 : 2 * PASSES], scalar1=-1.0, scalar2=1.0, op0=ALU.mult, op1=ALU.add
            )
            nc.vector.tensor_copy(out=mix[:], in_=mix_ps[:, :, 0 : 2 * PASSES])

            def turn(source, g, tag):
                piece, start = source[g]
                words = banks.tile([P, HALVES, B], F32, tag=tag)
                for h in range(HALVES):
                    for m in range(ROW_TILES):
                        nc.tensor.transpose(
                            words[:, h, P * m : P * (m + 1)],
                            piece[:, m, start : start + K_PASS].bitcast(F32)[:, h : K_PASS // 2 : HALVES],
                            ident_words[:],
                        )
                return words

            def by_index(words):
                return words[:].rearrange("p h b -> p (h b)").bitcast(BF16).rearrange("p (h b e) -> p h b e", h=HALVES, e=2)

            def mix_half(g, s, planes):
                sx_share = mixing.tile([P, PACK, B], F32)
                for t in range(PACK):
                    col = PASSES * s + g
                    nc.scalar.activation(
                        out=sx_share[:, t, :],
                        in_=turned_sx[g][:, t // 2, :, t % 2],
                        func=ACT.Copy,
                        scale=rest[:, t, col : col + 1],
                    )
                    nc.vector.scalar_tensor_tensor(
                        out=planes[:, s, t, :],
                        in0=turned_x[g][:, t // 2, :, t % 2],
                        scalar=mix[:, t, col : col + 1],
                        in1=sx_share[:, t, :],
                        op0=ALU.mult,
                        op1=ALU.add,
                    )

            def regroup(planes, grouped, s, engine):
                if engine == 0:
                    nc.gpsimd.tensor_scalar(
                        out=grouped[:, s],
                        in0=planes[:, s].rearrange("p t b -> p b t"),
                        scalar1=1.0,
                        scalar2=0.0,
                        op0=ALU.mult,
                        op1=ALU.add,
                    )
                else:
                    nc.vector.tensor_copy(
                        out=grouped[:, s].rearrange("p (c i) t -> p c t i", i=4),
                        in_=planes[:, s].rearrange("p t (c i) -> p c t i", i=4),
                    )

            def quantise(g, grouped, first_s, last_s):
                nc.vector.quantize_mx(
                    out=x_codes[:, g, first_s : last_s + 1].rearrange("p s b -> p (s b)").bitcast(FP8X4),
                    scales=x_scales[:, g, first_s : last_s + 1].rearrange("p s b -> p (s b)"),
                    in_=grouped[:, first_s : last_s + 1].rearrange("p s b t -> p (s b t)"),
                )

            turned_x, turned_sx = {}, {}
            planes_of, grouped_of = {}, {}

            def turn_both(g, tags):
                turned_sx[g] = by_index(turn(sx_sb, g, tags[0]))
                turned_x[g] = by_index(turn(x_sb, g, tags[1]))

            for g in range(PASSES):
                planes = mixing.tile([P, 2, PACK, B], BF16, bufs=4)
                grouped = mixing.tile([P, 2, B, PACK], BF16, bufs=4, align_bytes=64)
                planes_of[g], grouped_of[g] = planes, grouped

            def keys_of(j):
                pair = []
                for half in range(2):
                    k_ps = banks.tile([P, 2, B], F32, tag=("ka", "kb")[half])
                    for e in range(2):
                        c = 2 * half + e
                        for g in range(PASSES):
                            nc.tensor.matmul_mx(
                                out=k_ps[:, e, :],
                                lhsT=w_words[0, j][0][:, g, w_words[0, j][1] + P * c : w_words[0, j][1] + P * (c + 1)].bitcast(FP8X4),
                                lhsT_scale=w_scales[4 * g : P, 0, N_BLOCK * j + P * c : N_BLOCK * j + P * (c + 1)],
                                rhs=x_codes[:, g, 0, :].bitcast(FP8X4),
                                rhs_scale=x_scales[:, g, 0, :],
                                start=(g == 0),
                                stop=(g == PASSES - 1),
                            )
                    pair.append(k_ps)
                return pair

            g_of, p_of = {}, {}

            def new_states(j, keys, op):
                out = keep.tile([P, C_TILES, B], F32, tag=("g_turned" if op == ALU.subtract else "p_turned"), bufs=2)
                for half in range(2):
                    two = slice(2 * half, 2 * half + 2)
                    nc.vector.tensor_tensor(out=out[:, two], in0=w_turned[:, j % 2, two], in1=keys[half][:], op=op)
                (g_of if op == ALU.subtract else p_of)[j] = out

            def split(j, keys):
                new_states(j, keys, ALU.subtract)
                new_states(j, keys, ALU.max)

            def stage_states(i):
                j, m = divmod(i, ROW_TILES)
                ab_ps = banks.tile([P, 2, N_BLOCK], BF16, tag="ab")
                for s in range(2):
                    nc.tensor.matmul(
                        out=ab_ps[:, s, :], lhsT=ident[:], rhs=ab_sb[:, j // 2, s, m, N_BLOCK * (j % 2) : N_BLOCK * (j % 2 + 1)], start=True, stop=True
                    )
                return ab_ps


            def turned_sum(tag, left, right):
                total = banks.tile([P, N_BLOCK], F32, tag=tag)
                for c in range(C_TILES):
                    cols = slice(P * c, P * (c + 1))
                    nc.tensor.matmul(
                        out=total[:, cols], lhsT=left(c), rhs=ident_words[:],
                        start=True, stop=(right is None), is_transpose=True,
                    )
                    if right is not None:
                        nc.tensor.matmul(
                            out=total[:, cols], lhsT=right(c), rhs=ident_words[:],
                            start=False, stop=True, is_transpose=True,
                        )
                return total

            def exponents(i):
                j, m = divmod(i, ROW_TILES)
                rows = slice(P * m, P * (m + 1))
                first = keep.tile([P, 2, N_BLOCK], F32, bufs=3)
                second = keep.tile([P, 2, 2, N_BLOCK], F32, bufs=3)

                def gap(c):
                    ch = C_TILES * j + c
                    return shift_gap[:, ch : ch + 1].to_broadcast([P, P])

                for h, right in ((1, None), (0, gap)):
                    e_ps = turned_sum(("e0", "e1")[h], lambda c: g_of[j][:, c, rows], right)
                    nc.scalar.activation(out=first[:, h, :], in_=e_ps[:], func=ACT.Exp)
                    nc.scalar.activation(out=second[:, 1, h, :], in_=e_ps[:], func=ACT.Relu)
                nc.scalar.activation(out=second[:, 1], in_=second[:, 1], func=ACT.Exp, scale=-1.0)
                return first, second

            def emit_p(i):
                j, m = divmod(i, ROW_TILES)
                rows = slice(P * m, P * (m + 1))
                p_ps = turned_sum("p", lambda c: p_of[j][:, c, rows], None)
                p_out = work.tile([P, N_BLOCK], F32, bufs=STORE_BUFS_P)
                nc.scalar.copy(out=p_out[:], in_=p_ps[:])
                nc.sync.dma_start(out=out_4[rows, n_cols(j)], in_=p_out[:])

            def turn_shifts():
                shift_ps = banks.tile([P, P], BF16, tag="ka")
                nc.tensor.transpose(shift_ps[:], shift_rows[:], ident[:])
                spread = shift_ps[:, 0:32].rearrange("p (h c) -> p h c", h=2)
                decay = keep.tile([P, D // P], F32)
                nc.scalar.activation(out=decay[:], in_=spread[:, 1], func=ACT.Exp)
                nc.vector.tensor_scalar_mul(neg_decay[:], decay[:], -1.0)
                nc.vector.tensor_tensor(out=shift_gap[:], in0=spread[:, 0], in1=neg_decay[:], op=ALU.add)
                nc.vector.tensor_scalar_mul(shift_gap[:], shift_gap[:], -1.0)

            exps, states, values, results = {}, {}, {}, {}
            turn_both(0, ("p", "e2"))
            turn_both(1, ("e0", "e1"))
            mix_half(0, 1, planes_of[0])
            mix_half(0, 0, planes_of[0])
            turn_shifts()
            mix_half(1, 0, planes_of[1])
            turn_both(2, ("v", "ab"))
            regroup(planes_of[0], grouped_of[0], 1, 0)
            mix_half(2, 0, planes_of[2])
            turn_both(3, ("p", "e2"))
            mix_half(3, 0, planes_of[3])
            regroup(planes_of[0], grouped_of[0], 0, 0)
            regroup(planes_of[1], grouped_of[1], 0, 0)
            quantise(1, grouped_of[1], 0, 0)
            quantise(0, grouped_of[0], 0, 0)
            turn_states(0)
            regroup(planes_of[3], grouped_of[3], 0, 1)
            regroup(planes_of[2], grouped_of[2], 0, 0)
            quantise(2, grouped_of[2], 0, 0)
            quantise(3, grouped_of[3], 0, 0)
            quantise(0, grouped_of[0], 1, 1)
            mix_half(1, 1, planes_of[1])
            keys = keys_of(0)
            new_states(0, keys, ALU.subtract)
            mix_half(3, 1, planes_of[3])
            regroup(planes_of[1], grouped_of[1], 1, 0)
            regroup(planes_of[3], grouped_of[3], 1, 0)
            mix_half(2, 1, planes_of[2])
            new_states(0, keys, ALU.max)
            quantise(3, grouped_of[3], 1, 1)
            quantise(1, grouped_of[1], 1, 1)
            exps[0] = exponents(0)
            turn_states(1)
            regroup(planes_of[2], grouped_of[2], 1, 0)
            quantise(2, grouped_of[2], 1, 1)
            exps[1] = exponents(1)
            states[0] = stage_states(0)
            keys = keys_of(1)

        with tc.tile_pool(name="work", bufs=3, reuse_waits="tile") as work:

            def value_of(i):
                j, m = divmod(i, ROW_TILES)
                rows = slice(P * m, P * (m + 1))
                v_ps = banks.tile([P, N_BLOCK], F32, tag="v")
                for g in range(PASSES):
                    nc.tensor.matmul_mx(
                        out=v_ps[:],
                        lhsT=x_codes[:, g, 1, rows].bitcast(FP8X4),
                        lhsT_scale=x_scales[:, g, 1, rows],
                        rhs=w_words[1, j][0][:, g, w_words[1, j][1] : w_words[1, j][1] + N_BLOCK].bitcast(FP8X4),
                        rhs_scale=w_scales[4 * g : P, 1, n_cols(j)],
                        start=(g == 0),
                        stop=(g == PASSES - 1),
                    )
                return v_ps

            def state_terms(i, first, second, ab_ps):
                result = work.tile([P, 2, 2, N_BLOCK], F32, bufs=STORE_BUFS_AB)
                for h in range(2):
                    nc.vector.scalar_tensor_tensor(
                        out=result[:, :, h, :],
                        in0=first[:, h, :].unsqueeze(1).to_broadcast([P, 2, N_BLOCK]),
                        scalar=1.0,
                        in1=ab_ps[:],
                        op0=ALU.min,
                        op1=ALU.mult,
                    )
                add_and_store(i, 1, result, second)
                return result

            def value_terms(i, result, second, v_ps):
                nc.vector.tensor_tensor(
                    out=second[:, 0],
                    in0=second[:, 1],
                    in1=v_ps[:].unsqueeze(1).to_broadcast([P, 2, N_BLOCK]),
                    op=ALU.mult,
                )
                add_and_store(i, 0, result, second)

            def add_and_store(i, s, result, second):
                count = 2 * i + 1 - s
                if count >= 2 * UNITS - VECTOR_SUMS and not late:
                    late_sums.append((i, s, result, second))
                    return
                j, m = divmod(i, ROW_TILES)
                rows = slice(P * m, P * (m + 1))
                adder = nc.vector if late else nc.gpsimd
                adder.tensor_tensor(out=result[:, s], in0=result[:, s], in1=second[:, s], op=ALU.add)
                for h, out in enumerate(((out_0, out_2), (out_1, out_3))[s]):
                    nc.sync.dma_start(out=out[rows, n_cols(j)], in_=result[:, s, h, :])

            late = []
            late_sums = []
            for j in range(N_BLOCKS):
                first_unit, second_unit = ROW_TILES * j, ROW_TILES * j + 1
                more = j + 1 < N_BLOCKS
                values[first_unit] = value_of(first_unit)
                if j + 2 < N_BLOCKS:
                    turn_states(j + 2)
                emit_p(first_unit)
                results[first_unit] = state_terms(first_unit, exps[first_unit][0], exps[first_unit][1], states[first_unit])
                if more:
                    new_states(j + 1, keys, ALU.subtract)
                states[second_unit] = stage_states(second_unit)
                if more:
                    exps[first_unit + 2] = exponents(first_unit + 2)
                value_terms(first_unit, results[first_unit], exps[first_unit][1], values[first_unit])
                values[second_unit] = value_of(second_unit)
                emit_p(second_unit)
                results[second_unit] = state_terms(
                    second_unit, exps[second_unit][0], exps[second_unit][1], states[second_unit]
                )
                if more:
                    new_states(j + 1, keys, ALU.max)
                    states[first_unit + 2] = stage_states(first_unit + 2)
                    if j + 2 < N_BLOCKS:
                        keys = keys_of(j + 2)
                    exps[second_unit + 2] = exponents(second_unit + 2)
                value_terms(second_unit, results[second_unit], exps[second_unit][1], values[second_unit])
            late.append(True)
            for i, s, result, second in late_sums:
                add_and_store(i, s, result, second)
